import numpy as np
import ml_dtypes


def mxq(x, axis, fmt="e4m3"):
    dtype, down = {"e4m3": (ml_dtypes.float8_e4m3fn, 7), "e5m2": (ml_dtypes.float8_e5m2, 14)}[fmt]
    v = np.moveaxis(np.asarray(x, np.float32).astype(ml_dtypes.bfloat16).astype(np.float64), axis, -1)
    blocks = v.reshape(v.shape[:-1] + (-1, 32))
    amax = np.abs(blocks).max(-1, keepdims=True)
    byte = np.maximum(np.where(amax > 0, np.frexp(amax)[1] - 1 + 127, 0) - down, 1)
    scale = np.exp2(byte - 127.0)
    codes = (blocks / scale).astype(np.float32).astype(dtype).astype(np.float64)
    return np.moveaxis((codes * scale).reshape(v.shape), -1, axis)


WIDE = False


def mx_kscale(k):
    if not WIDE:
        return np.ones(k)
    levels = np.array([10, -10, 5, -5, 0])
    if k % 512:
        return np.exp2(np.random.permutation(np.resize(levels, k // 32))).repeat(32)
    a = np.empty((k // 512, 16))
    for p in range(k // 512):
        a[p, :8] = np.random.permutation(np.resize(levels, 8))
        for g in range(8):
            far = levels[np.abs(levels - a[p, g]) >= 10]
            a[p, g + 8] = far[np.random.randint(len(far))]
    return np.exp2(a.ravel()).repeat(32)


BF16 = ml_dtypes.bfloat16


def bf(x):
    return np.asarray(x, np.float32).astype(BF16)


def f64(x):
    return np.asarray(x).astype(np.float64)


B, D, N, L = 16384, 512, 128, 4
BN_EPS = 1e-5


def setup_inputs():
    t = mx_kscale(D)
    return {"h_lin": bf(np.random.standard_normal((B, D)) * 0.6 + np.random.standard_normal(D) * 0.5),
            "gamma": bf(np.random.uniform(0.5, 1.5, D) * t),
            "beta": bf(np.random.standard_normal(D) * 0.2 * t),
            "w": bf(np.random.standard_normal((D, N)) / np.sqrt(D) / t[:, None]),
            "b": bf(np.random.standard_normal(N) * 0.2)}


def reference(h_lin, gamma, beta, w, b):
    z = f64(h_lin)
    mu = z.mean(0)
    var = ((z - mu) ** 2).mean(0)
    h = np.maximum((z - mu) / np.sqrt(var + BN_EPS) * f64(gamma) + f64(beta), 0.0)
    return (mxq(h, 1, "e4m3") @ mxq(f64(w), 0, "e4m3")) + f64(b)

@@ -1,0 +1,296 @@
+from contextlib import ExitStack
+
+import concourse.masks as masks
+import concourse.mybir as mybir
+
+F32 = mybir.dt.float32
+BF16 = mybir.dt.bfloat16
+U32 = mybir.dt.uint32
+U8 = mybir.dt.uint8
+FP8X4 = mybir.dt.float8_e4m3fn_x4
+FUNC = mybir.ActivationFunctionType
+ALU = mybir.AluOpType
+AXIS = mybir.AxisListType
+
+P = 128
+PACK = 4
+ROWS = 16384
+K = 512
+N_OUT = 128
+BN_EPS = 1e-5
+
+BLOCKS = ROWS // P
+GROUP = 4
+GROUPS = BLOCKS // GROUP
+GROUP_ROWS = GROUP * P
+HALF_K = K // 2
+BN_STATS_MAX = 512
+BN_CALLS = 2 * GROUP_ROWS // BN_STATS_MAX
+ONES = 2
+GPSIMD_BLOCKS = 2
+EARLY_GROUPS = 24
+AHEAD = 2
+
+FLOPS = 2 * ROWS * K * N_OUT
+
+
+def tile_customnetwork_pa_t_kernel(tc, h_lin, gamma, beta, w, b, out):
+    nc = tc.nc
+    x_dram = h_lin.rearrange("(p a) k -> p a k", a=BLOCKS)
+    out_dram = out.rearrange("(p a) n -> p a n", a=BLOCKS)
+
+    with ExitStack() as stack:
+        const = stack.enter_context(tc.tile_pool(name="const", bufs=1))
+        resident = stack.enter_context(tc.tile_pool(name="resident", bufs=GROUPS))
+        unread = stack.enter_context(tc.tile_pool(name="unread", bufs=4))
+        stage = stack.enter_context(tc.tile_pool(name="stage", bufs=3))
+        results = stack.enter_context(tc.tile_pool(name="results", bufs=4))
+        psum_x = stack.enter_context(tc.psum_pool(name="psum_x", bufs=6))
+        psum_acc = stack.enter_context(tc.psum_pool(name="psum_acc", bufs=2))
+        stack.enter_context(tc.manual_schedule())
+
+        eps = const.tile([P, 1], F32)
+        nc.vector.memset(eps[:], BN_EPS)
+        ones = const.tile([P, ONES], BF16)
+        nc.vector.memset(ones[:], 1.0)
+        ones_f32 = const.tile([P, ONES], F32)
+        nc.vector.memset(ones_f32[:], 1.0)
+        partition_sums = const.tile([P, GPSIMD_BLOCKS, HALF_K], F32)
+        nc.gpsimd.memset(partition_sums[:], 0.0)
+        gb_rows = const.tile([P, K], BF16)
+        nc.vector.memset(gb_rows[:], 0.0)
+        ident = const.tile([P, P], F32)
+        masks.make_identity(nc, ident[:])
+
+        nc.scalar.dma_start(out=gb_rows[0:1, :], in_=gamma.unsqueeze(0))
+        nc.scalar.dma_start(out=gb_rows[1:2, :], in_=beta.unsqueeze(0))
+        w_planes = const.tile([P, PACK, N_OUT], BF16)
+        nc.scalar.dma_start(out=w_planes[:], in_=w.rearrange("(p t) n -> p t n", t=PACK))
+        warm = const.tile([P, 1], F32)
+        nc.scalar.activation(out=warm[:], in_=eps[:], func=FUNC.Sqrt)
+
+        x_tiles = []
+        for g in range(GROUPS):
+            x_g = resident.tile([P, GROUP, K], BF16, name="x_g")
+            if g == 0:
+                for j in range(GROUP):
+                    nc.sync.dma_start(out=x_g[:, j, :], in_=x_dram[:, j, :])
+            else:
+                nc.sync.dma_start(out=x_g[:], in_=x_dram[:, g * GROUP : (g + 1) * GROUP, :])
+            x_tiles.append(x_g)
+        b_rows = const.tile([P, N_OUT], BF16)
+        nc.sync.dma_start(out=b_rows[:], in_=b.partition_broadcast(P))
+
+        def transpose_half(g, u):
+            words = x_tiles[g][:].bitcast(F32)
+            xt = psum_x.tile([P, GROUP_ROWS], F32, name="xt")
+            for j in range(GROUP):
+                nc.tensor.transpose(
+                    xt[:, j * P : (j + 1) * P], words[:, j, u : HALF_K : 2], ident[:]
+                )
+            return xt
+
+        def one_k(xt, e):
+            return xt[:].bitcast(BF16).rearrange("p (r e) -> p r e", e=2)[:, :, e]
+
+        low_calls = GROUPS * BN_CALLS
+        early_calls = EARLY_GROUPS * BN_CALLS
+        early_rows = EARLY_GROUPS * GROUP_ROWS
+        low_stats = const.tile([P, low_calls + 1, 2, 3], F32)
+        nc.vector.memset(low_stats[:, low_calls, :, :], float(early_rows))
+        shift_stats = const.tile([P, 2, 3], F32)
+        neg_shift = const.tile([P, 2], F32)
+        square_sums = const.tile([P, 2, GROUPS], F32)
+        plain_sums = []
+        for e in range(2):
+            plain_sum = psum_acc.tile([P, ONES], F32, name="acc")
+            plain_sums.append(plain_sum)
+
+        for g in range(GROUPS):
+            xt_low = transpose_half(g, 0)
+            for i in range(BN_CALLS):
+                nc.vector.bn_stats(
+                    out=low_stats[:, g * BN_CALLS + i, :, :].rearrange("p e s -> p (e s)"),
+                    in_=xt_low[:].bitcast(BF16)[:, i * BN_STATS_MAX : (i + 1) * BN_STATS_MAX],
+                )
+            if g == EARLY_GROUPS - 1:
+                for e in range(2):
+                    nc.vector.bn_aggr(
+                        out=low_stats[:, low_calls, e, 1:3], in_=low_stats[:, 0:early_calls, e, :]
+                    )
+                nc.vector.tensor_scalar(
+                    out=low_stats[:, low_calls, :, 2],
+                    in0=low_stats[:, low_calls, :, 2],
+                    scalar1=float(early_rows),
+                    scalar2=None,
+                    op0=ALU.mult,
+                )
+            xt_high = transpose_half(g, 1)
+            if g == 0:
+                nc.vector.bn_stats(
+                    out=shift_stats[:].rearrange("p e s -> p (e s)"),
+                    in_=xt_high[:].bitcast(BF16)[:, 0:BN_STATS_MAX],
+                )
+                nc.vector.tensor_scalar(
+                    out=neg_shift[:], in0=shift_stats[:, :, 1], scalar1=-1.0, scalar2=None, op0=ALU.mult
+                )
+            for e in range(2):
+                squares = unread.tile([P, GROUP_ROWS], BF16, name="squares")
+                nc.scalar.activation(
+                    out=squares[:],
+                    in_=one_k(xt_high, e),
+                    func=FUNC.Square,
+                    bias=neg_shift[:, e : e + 1],
+                    scale=1.0,
+                    accum_out=square_sums[:, e, g : g + 1],
+                )
+            nc.gpsimd.tensor_tensor(
+                out=partition_sums[:].rearrange("p j (m e) -> p j m e", e=2),
+                in0=partition_sums[:].rearrange("p j (m e) -> p j m e", e=2),
+                in1=x_tiles[g][:, 0:GPSIMD_BLOCKS, :].rearrange("p j (m t) -> p j m t", t=PACK)[:, :, :, 2:4],
+                op=ALU.add,
+            )
+            for e in range(2):
+                for j in range(GPSIMD_BLOCKS, GROUP):
+                    nc.tensor.matmul(
+                        out=plain_sums[e][:],
+                        lhsT=x_tiles[g][:, j, :].rearrange("p (m t) -> p m t", t=PACK)[:, :, 2 + e],
+                        rhs=ones[:],
+                        start=(g == 0 and j == GPSIMD_BLOCKS),
+                        stop=False,
+                    )
+
+        gb_t = psum_x.tile([P, GROUP_ROWS], F32, name="xt")
+        for u in range(2):
+            nc.tensor.transpose(gb_t[:, u * P : (u + 1) * P], gb_rows[:].bitcast(F32)[:, u : HALF_K : 2], ident[:])
+        gamma_beta = const.tile([P, 2, PACK], F32)
+        for u in range(2):
+            nc.vector.tensor_copy(
+                out=gamma_beta[:, :, 2 * u : 2 * u + 2],
+                in_=gb_t[:].bitcast(BF16)[:, 2 * u * P : 2 * u * P + 4].rearrange("p (g e) -> p g e", e=2),
+            )
+
+        for e in range(2):
+            for j in range(GPSIMD_BLOCKS):
+                nc.tensor.matmul(
+                    out=plain_sums[e][:],
+                    lhsT=partition_sums[:, j, :].rearrange("p (m e) -> p m e", e=2)[:, :, e],
+                    rhs=ones_f32[:],
+                    start=False,
+                    stop=(j == GPSIMD_BLOCKS - 1),
+                )
+
+        xt_of = {}
+        for g in range(AHEAD):
+            xt_of[g] = [transpose_half(g, 0), transpose_half(g, 1)]
+
+        mean_var = const.tile([P, PACK, 2], F32)
+        for e in range(2):
+            nc.vector.bn_aggr(out=mean_var[:, e, :], in_=low_stats[:, early_calls : low_calls + 1, e, :])
+        for e in range(2):
+            nc.vector.tensor_scalar(
+                out=mean_var[:, 2 + e, 0:1], in0=plain_sums[e][:, 0:1], scalar1=1.0 / ROWS, scalar2=None, op0=ALU.mult
+            )
+        off_centre = const.tile([P, 2], F32)
+        nc.vector.tensor_tensor(out=off_centre[:], in0=mean_var[:, 2:4, 0], in1=neg_shift[:], op=ALU.add)
+        off_centre_sq = const.tile([P, 2], F32)
+        nc.vector.tensor_tensor(out=off_centre_sq[:], in0=off_centre[:], in1=off_centre[:], op=ALU.mult)
+        high_square_sum = const.tile([P, 2], F32)
+        nc.vector.tensor_reduce(out=high_square_sum[:], in_=square_sums[:], axis=AXIS.X, op=ALU.add)
+        nc.vector.scalar_tensor_tensor(
+            out=mean_var[:, 2:4, 1],
+            in0=high_square_sum[:],
+            scalar=1.0 / ROWS,
+            in1=off_centre_sq[:],
+            op0=ALU.mult,
+            op1=ALU.subtract,
+        )
+        std = const.tile([P, PACK], F32)
+        nc.scalar.activation(out=std[:], in_=mean_var[:, :, 1], func=FUNC.Sqrt, bias=eps[:], scale=1.0)
+        inv_std = const.tile([P, PACK], F32)
+        nc.vector.reciprocal(out=inv_std[:], in_=std[:])
+        scale_k = const.tile([P, PACK], F32)
+        nc.vector.tensor_tensor(out=scale_k[:], in0=gamma_beta[:, 0, :], in1=inv_std[:], op=ALU.mult)
+        mean_scaled = const.tile([P, PACK], F32)
+        nc.vector.tensor_tensor(out=mean_scaled[:], in0=mean_var[:, :, 0], in1=scale_k[:], op=ALU.mult)
+        offset_k = const.tile([P, PACK], F32)
+        nc.vector.tensor_tensor(out=offset_k[:], in0=gamma_beta[:, 1, :], in1=mean_scaled[:], op=ALU.subtract)
+
+        w_grouped = const.tile([P, N_OUT, PACK], BF16, align_bytes=64)
+        nc.vector.tensor_copy(out=w_grouped[:], in_=w_planes[:].rearrange("p t n -> p n t"))
+        w_codes = const.tile([P, N_OUT], U32, align_bytes=64)
+        w_scales = const.tile([P, N_OUT], U8, align_bytes=64)
+        nc.vector.quantize_mx(
+            out=w_codes[:].bitcast(FP8X4),
+            scales=w_scales[:],
+            in_=w_grouped[:].rearrange("p n t -> p (n t)"),
+        )
+
+        planes_of = {}
+        grouped_of = {}
+        acc_of = {}
+
+        def normalise(g):
+            planes = stage.tile([P, PACK, GROUP_ROWS], BF16, name="planes")
+            for u in range(2):
+                for e in range(2):
+                    t = 2 * u + e
+                    nc.scalar.activation(
+                        out=planes[:, t, :],
+                        in_=one_k(xt_of[g][u], e),
+                        func=FUNC.Relu,
+                        bias=offset_k[:, t : t + 1],
+                        scale=scale_k[:, t : t + 1],
+                    )
+            planes_of[g] = planes
+
+        def interleave(g):
+            grouped = stage.tile([P, GROUP_ROWS, PACK], BF16, name="grouped", align_bytes=64)
+            nc.vector.tensor_copy(
+                out=grouped[:].rearrange("p (c i) t -> p c t i", i=4),
+                in_=planes_of[g][:].rearrange("p t (c i) -> p c t i", i=4),
+            )
+            grouped_of[g] = grouped
+
+        def quantise_and_multiply(g):
+            codes = stage.tile([P, GROUP_ROWS], U32, name="codes", align_bytes=64)
+            scales = stage.tile([P, GROUP_ROWS], U8, name="scales", align_bytes=64)
+            nc.vector.quantize_mx(
+                out=codes[:].bitcast(FP8X4),
+                scales=scales[:],
+                in_=grouped_of[g][:].rearrange("p r t -> p (r t)"),
+            )
+            acc = psum_acc.tile([P, GROUP, N_OUT], F32, name="acc")
+            for j in range(GROUP):
+                block = slice(j * P, (j + 1) * P)
+                nc.tensor.matmul_mx(
+                    out=acc[:, j, :],
+                    lhsT=codes[:, block].bitcast(FP8X4),
+                    lhsT_scale=scales[:, block],
+                    rhs=w_codes[:].bitcast(FP8X4),
+                    rhs_scale=w_scales[:],
+                    start=True,
+                    stop=True,
+                )
+            acc_of[g] = acc
+
+        def add_bias_and_store(g):
+            result = results.tile([P, GROUP, N_OUT], F32, name="result")
+            nc.vector.tensor_tensor(
+                out=result[:],
+                in0=acc_of[g][:],
+                in1=b_rows[:].unsqueeze(1).to_broadcast([P, GROUP, N_OUT]),
+                op=ALU.add,
+            )
+            nc.sync.dma_start(out=out_dram[:, g * GROUP : (g + 1) * GROUP, :], in_=result[:])
+
+        for s in range(GROUPS + 2):
+            if s + AHEAD < GROUPS:
+                xt_of[s + AHEAD] = [transpose_half(s + AHEAD, 0), transpose_half(s + AHEAD, 1)]
+            if s < GROUPS:
+                normalise(s)
+                interleave(s)
+            if 1 <= s <= GROUPS:
+                quantise_and_multiply(s - 1)
+            if s >= 2:
+                add_bias_and_store(s - 2)

@@ -27,9 +27,24 @@ HALF_K = K // 2
 BN_STATS_MAX = 512
 BN_CALLS = 2 * GROUP_ROWS // BN_STATS_MAX
 ONES = 2
-GPSIMD_BLOCKS = 2
-EARLY_GROUPS = 24
 AHEAD = 2
+
+GPSIMD_GROUPS = (1, 5, 13, 21)
+BANK_GROUPS = [g for g in range(GROUPS) if g not in GPSIMD_GROUPS]
+LAST = BANK_GROUPS[-1]
+EARLY = 24
+
+
+def owner_of_high(i):
+    if i == len(BANK_GROUPS) - 1 or (i % 4 == 0 and i < EARLY):
+        return "vector"
+    return "scalar_twice" if i % 4 in (2, 3) else "scalar"
+
+
+VECTOR_HIGH = [i for i in range(len(BANK_GROUPS)) if owner_of_high(i) == "vector"]
+SCALAR_HIGH = [i for i in range(len(BANK_GROUPS)) if owner_of_high(i) != "vector"]
+TWICE_HIGH = [i for i in range(len(BANK_GROUPS)) if owner_of_high(i) == "scalar_twice"]
+ONCE_HIGH = [i for i in range(len(BANK_GROUPS)) if owner_of_high(i) == "scalar"]
 
 FLOPS = 2 * ROWS * K * N_OUT
 
@@ -55,8 +70,6 @@ def tile_customnetwork_pa_t_kernel(tc, h_lin, gamma, beta, w, b, out):
         nc.vector.memset(ones[:], 1.0)
         ones_f32 = const.tile([P, ONES], F32)
         nc.vector.memset(ones_f32[:], 1.0)
-        partition_sums = const.tile([P, GPSIMD_BLOCKS, HALF_K], F32)
-        nc.gpsimd.memset(partition_sums[:], 0.0)
         gb_rows = const.tile([P, K], BF16)
         nc.vector.memset(gb_rows[:], 0.0)
         ident = const.tile([P, P], F32)
@@ -90,95 +103,212 @@ def tile_customnetwork_pa_t_kernel(tc, h_lin, gamma, beta, w, b, out):
                 )
             return xt
 
-        def one_k(xt, e):
-            return xt[:].bitcast(BF16).rearrange("p (r e) -> p r e", e=2)[:, :, e]
+        def one_k(xt, e, columns=slice(0, GROUP_ROWS)):
+            return xt[:].bitcast(BF16).rearrange("p (r e) -> p r e", e=2)[:, columns, e]
 
-        low_calls = GROUPS * BN_CALLS
-        early_calls = EARLY_GROUPS * BN_CALLS
-        early_rows = EARLY_GROUPS * GROUP_ROWS
-        low_stats = const.tile([P, low_calls + 1, 2, 3], F32)
-        nc.vector.memset(low_stats[:, low_calls, :, :], float(early_rows))
-        shift_stats = const.tile([P, 2, 3], F32)
+        def column_sum(bank, column, g, t):
+            for j in range(GROUP):
+                nc.tensor.matmul(
+                    out=bank[:, column * ONES : (column + 1) * ONES],
+                    lhsT=x_tiles[g][:, j, :].rearrange("p (m t) -> p m t", t=PACK)[:, :, t],
+                    rhs=ones[:],
+                    start=(j == 0),
+                    stop=(j == GROUP - 1),
+                )
+
+        low_calls = len(BANK_GROUPS) * BN_CALLS
+        early_calls = EARLY * BN_CALLS
+        early_high = len(VECTOR_HIGH) - 1
+        high_late = low_calls - BN_CALLS
+        merged, gpsimd_slot, scalar_slot = low_calls, low_calls + 1, low_calls + 2
+        stats = const.tile([P, 2, low_calls + 3, 2, 3], F32)
+        early_rows = (EARLY * GROUP_ROWS, early_high * GROUP_ROWS)
+        gpsimd_rows = len(GPSIMD_GROUPS) * GROUP_ROWS
+        scalar_rows = len(SCALAR_HIGH) * GROUP_ROWS
+        for u in range(2):
+            nc.vector.memset(stats[:, u, merged, :, :], float(early_rows[u]))
+        nc.vector.memset(stats[:, :, gpsimd_slot, :, :], float(gpsimd_rows))
+        nc.vector.memset(stats[:, 1, scalar_slot, :, :], float(scalar_rows))
+
         neg_shift = const.tile([P, 2], F32)
-        square_sums = const.tile([P, 2, GROUPS], F32)
-        plain_sums = []
-        for e in range(2):
-            plain_sum = psum_acc.tile([P, ONES], F32, name="acc")
-            plain_sums.append(plain_sum)
+        square_sums = const.tile([P, 2, len(SCALAR_HIGH)], F32)
+        twice_sums = const.tile([P, 2, len(TWICE_HIGH)], F32)
+        once_bank = psum_acc.tile([P, GROUP_ROWS], F32, name="acc")
+        gpsimd_bank = psum_acc.tile([P, GROUP_ROWS], F32, name="acc")
+        row_squares = const.tile([P, GROUP, K], F32)
+        more_squares = const.tile([P, GROUP, K], F32)
+        gamma_mean = const.tile([P, 2, PACK], F32)
+        beta_k = const.tile([P, PACK], F32)
+        w_grouped = const.tile([P, N_OUT, PACK], BF16, align_bytes=64)
+        w_codes = const.tile([P, N_OUT], U32, align_bytes=64)
+        w_scales = const.tile([P, N_OUT], U8, align_bytes=64)
 
-        for g in range(GROUPS):
-            xt_low = transpose_half(g, 0)
+        def bn_bank(xt, u, first_slot):
             for i in range(BN_CALLS):
                 nc.vector.bn_stats(
-                    out=low_stats[:, g * BN_CALLS + i, :, :].rearrange("p e s -> p (e s)"),
-                    in_=xt_low[:].bitcast(BF16)[:, i * BN_STATS_MAX : (i + 1) * BN_STATS_MAX],
+                    out=stats[:, u, first_slot + i, :, :].rearrange("p e s -> p (e s)"),
+                    in_=xt[:].bitcast(BF16)[:, i * BN_STATS_MAX : (i + 1) * BN_STATS_MAX],
                 )
-            if g == EARLY_GROUPS - 1:
-                for e in range(2):
-                    nc.vector.bn_aggr(
-                        out=low_stats[:, low_calls, e, 1:3], in_=low_stats[:, 0:early_calls, e, :]
-                    )
-                nc.vector.tensor_scalar(
-                    out=low_stats[:, low_calls, :, 2],
-                    in0=low_stats[:, low_calls, :, 2],
-                    scalar1=float(early_rows),
-                    scalar2=None,
-                    op0=ALU.mult,
-                )
-            xt_high = transpose_half(g, 1)
-            if g == 0:
-                nc.vector.bn_stats(
-                    out=shift_stats[:].rearrange("p e s -> p (e s)"),
-                    in_=xt_high[:].bitcast(BF16)[:, 0:BN_STATS_MAX],
-                )
-                nc.vector.tensor_scalar(
-                    out=neg_shift[:], in0=shift_stats[:, :, 1], scalar1=-1.0, scalar2=None, op0=ALU.mult
-                )
+
+        def merge_early(u, calls):
             for e in range(2):
-                squares = unread.tile([P, GROUP_ROWS], BF16, name="squares")
-                nc.scalar.activation(
-                    out=squares[:],
-                    in_=one_k(xt_high, e),
-                    func=FUNC.Square,
-                    bias=neg_shift[:, e : e + 1],
-                    scale=1.0,
-                    accum_out=square_sums[:, e, g : g + 1],
-                )
-            nc.gpsimd.tensor_tensor(
-                out=partition_sums[:].rearrange("p j (m e) -> p j m e", e=2),
-                in0=partition_sums[:].rearrange("p j (m e) -> p j m e", e=2),
-                in1=x_tiles[g][:, 0:GPSIMD_BLOCKS, :].rearrange("p j (m t) -> p j m t", t=PACK)[:, :, :, 2:4],
+                nc.vector.bn_aggr(out=stats[:, u, merged, e, 1:3], in_=stats[:, u, 0:calls, e, :])
+            nc.vector.tensor_scalar(
+                out=stats[:, u, merged, :, 2],
+                in0=stats[:, u, merged, :, 2],
+                scalar1=float(early_rows[u]),
+                scalar2=None,
+                op0=ALU.mult,
+            )
+
+        def squares_on_gpsimd(g):
+            first = g == GPSIMD_GROUPS[0]
+            squares = row_squares if first else more_squares
+            nc.gpsimd.tensor_tensor(out=squares[:], in0=x_tiles[g][:], in1=x_tiles[g][:], op=ALU.mult)
+            if not first:
+                nc.gpsimd.tensor_tensor(out=row_squares[:], in0=row_squares[:], in1=more_squares[:], op=ALU.add)
+            if g == GPSIMD_GROUPS[-1]:
+                for half in (2, 1):
+                    nc.gpsimd.tensor_tensor(
+                        out=row_squares[:, 0:half, :],
+                        in0=row_squares[:, 0:half, :],
+                        in1=row_squares[:, half : 2 * half, :],
+                        op=ALU.add,
+                    )
+
+        def close_gpsimd():
+            sums = const.tile([P, 2, 2], F32, name="g_sums")
+            nc.vector.tensor_reduce(
+                out=sums[:],
+                in_=gpsimd_bank[:, 0 : len(GPSIMD_GROUPS) * PACK * ONES].rearrange(
+                    "p (g u e o) -> p u e g o", u=2, e=2, o=ONES
+                )[:, :, :, :, 0],
+                axis=AXIS.X,
                 op=ALU.add,
             )
-            for e in range(2):
-                for j in range(GPSIMD_BLOCKS, GROUP):
-                    nc.tensor.matmul(
-                        out=plain_sums[e][:],
-                        lhsT=x_tiles[g][:, j, :].rearrange("p (m t) -> p m t", t=PACK)[:, :, 2 + e],
-                        rhs=ones[:],
-                        start=(g == 0 and j == GPSIMD_BLOCKS),
-                        stop=False,
-                    )
-
-        gb_t = psum_x.tile([P, GROUP_ROWS], F32, name="xt")
-        for u in range(2):
-            nc.tensor.transpose(gb_t[:, u * P : (u + 1) * P], gb_rows[:].bitcast(F32)[:, u : HALF_K : 2], ident[:])
-        gamma_beta = const.tile([P, 2, PACK], F32)
-        for u in range(2):
-            nc.vector.tensor_copy(
-                out=gamma_beta[:, :, 2 * u : 2 * u + 2],
-                in_=gb_t[:].bitcast(BF16)[:, 2 * u * P : 2 * u * P + 4].rearrange("p (g e) -> p g e", e=2),
+            mean = stats[:, :, gpsimd_slot, :, 1]
+            nc.vector.tensor_scalar(out=mean, in0=sums[:], scalar1=1.0 / gpsimd_rows, scalar2=None, op0=ALU.mult)
+            mean_sums = const.tile([P, 2, 2], F32, name="g_mean_sums")
+            nc.vector.tensor_tensor(out=mean_sums[:], in0=mean, in1=sums[:], op=ALU.mult)
+            spread = const.tile([P, 2, 2], F32, name="g_spread")
+            base = len(GPSIMD_GROUPS) * PACK
+            nc.vector.tensor_tensor(
+                out=spread[:],
+                in0=gpsimd_bank[:, base * ONES : (base + PACK) * ONES].rearrange(
+                    "p (u e o) -> p u e o", u=2, o=ONES
+                )[:, :, :, 0],
+                in1=mean_sums[:],
+                op=ALU.subtract,
+            )
+            nc.vector.tensor_scalar(
+                out=stats[:, :, gpsimd_slot, :, 2], in0=spread[:], scalar1=0.0, scalar2=None, op0=ALU.max
             )
 
-        for e in range(2):
-            for j in range(GPSIMD_BLOCKS):
-                nc.tensor.matmul(
-                    out=plain_sums[e][:],
-                    lhsT=partition_sums[:, j, :].rearrange("p (m e) -> p m e", e=2)[:, :, e],
-                    rhs=ones_f32[:],
-                    start=False,
-                    stop=(j == GPSIMD_BLOCKS - 1),
+        def close_scalar():
+            once = const.tile([P, 2], F32, name="s_once")
+            nc.vector.tensor_reduce(
+                out=once[:],
+                in_=once_bank[:, 0 : len(ONCE_HIGH) * 2 * ONES].rearrange(
+                    "p (i e o) -> p e i o", e=2, o=ONES
+                )[:, :, :, 0],
+                axis=AXIS.X,
+                op=ALU.add,
+            )
+            twice = const.tile([P, 2], F32, name="s_twice")
+            nc.vector.tensor_reduce(out=twice[:], in_=twice_sums[:], axis=AXIS.X, op=ALU.add)
+            squares = const.tile([P, 2], F32, name="s_squares")
+            nc.vector.tensor_reduce(out=squares[:], in_=square_sums[:], axis=AXIS.X, op=ALU.add)
+            sums = const.tile([P, 2], F32, name="s_sums")
+            nc.vector.tensor_tensor(out=sums[:], in0=once[:], in1=twice[:], op=ALU.add)
+            mean = stats[:, 1, scalar_slot, :, 1]
+            nc.vector.tensor_scalar(out=mean, in0=sums[:], scalar1=1.0 / scalar_rows, scalar2=None, op0=ALU.mult)
+            off = const.tile([P, 2], F32, name="s_off")
+            nc.vector.tensor_tensor(out=off[:], in0=mean, in1=neg_shift[:], op=ALU.add)
+            off_sq = const.tile([P, 2], F32, name="s_off_sq")
+            nc.vector.tensor_tensor(out=off_sq[:], in0=off[:], in1=off[:], op=ALU.mult)
+            spread = const.tile([P, 2], F32, name="s_spread")
+            nc.vector.scalar_tensor_tensor(
+                out=spread[:], in0=off_sq[:], scalar=-float(scalar_rows), in1=squares[:], op0=ALU.mult, op1=ALU.add
+            )
+            nc.vector.tensor_scalar(
+                out=stats[:, 1, scalar_slot, :, 2], in0=spread[:], scalar1=0.0, scalar2=None, op0=ALU.max
+            )
+
+        for g in range(GROUPS):
+            if g in GPSIMD_GROUPS:
+                squares_on_gpsimd(g)
+                for t in range(PACK):
+                    column_sum(gpsimd_bank, GPSIMD_GROUPS.index(g) * PACK + t, g, t)
+                continue
+            i = BANK_GROUPS.index(g)
+            owner = owner_of_high(i)
+            if g == LAST:
+                for t in range(PACK):
+                    nc.tensor.matmul(
+                        out=gpsimd_bank[
+                            :, (len(GPSIMD_GROUPS) * PACK + t) * ONES : (len(GPSIMD_GROUPS) * PACK + t + 1) * ONES
+                        ],
+                        lhsT=row_squares[:, 0, :].rearrange("p (m t) -> p m t", t=PACK)[:, :, t],
+                        rhs=ones_f32[:],
+                        start=True,
+                        stop=True,
+                    )
+            xt_low = transpose_half(g, 0)
+            xt_high = transpose_half(g, 1)
+            if g == LAST:
+                close_scalar()
+                close_gpsimd()
+            bn_bank(xt_low, 0, i * BN_CALLS)
+            if owner == "vector":
+                v = VECTOR_HIGH.index(i)
+                bn_bank(xt_high, 1, high_late if g == LAST else v * BN_CALLS)
+                if i == 0:
+                    nc.vector.tensor_scalar(
+                        out=neg_shift[:], in0=stats[:, 1, 0, :, 1], scalar1=-1.0, scalar2=None, op0=ALU.mult
+                    )
+            else:
+                s = SCALAR_HIGH.index(i)
+                for e in range(2):
+                    squares = unread.tile([P, GROUP_ROWS], BF16, name="squares")
+                    nc.scalar.activation(
+                        out=squares[:],
+                        in_=one_k(xt_high, e),
+                        func=FUNC.Square,
+                        bias=neg_shift[:, e : e + 1],
+                        scale=1.0,
+                        accum_out=square_sums[:, e, s : s + 1],
+                    )
+                    if owner == "scalar_twice":
+                        d = TWICE_HIGH.index(i)
+                        copy = unread.tile([P, GROUP_ROWS], BF16, name="squares")
+                        nc.scalar.activation(
+                            out=copy[:],
+                            in_=one_k(xt_high, e),
+                            func=FUNC.Identity,
+                            accum_out=twice_sums[:, e, d : d + 1],
+                        )
+                    else:
+                        column_sum(once_bank, ONCE_HIGH.index(i) * 2 + e, g, 2 + e)
+            if i == 2:
+                gb_t = psum_x.tile([P, GROUP_ROWS], F32, name="xt")
+                for u in range(2):
+                    nc.tensor.transpose(
+                        gb_t[:, u * P : (u + 1) * P], gb_rows[:].bitcast(F32)[:, u : HALF_K : 2], ident[:]
+                    )
+                for u in range(2):
+                    pairs = gb_t[:].bitcast(BF16)[:, 2 * u * P : 2 * u * P + 4]
+                    nc.vector.tensor_copy(out=gamma_mean[:, 0, 2 * u : 2 * u + 2], in_=pairs[:, 0:2])
+                    nc.vector.tensor_copy(out=beta_k[:, 2 * u : 2 * u + 2], in_=pairs[:, 2:4])
+                nc.vector.tensor_copy(out=w_grouped[:], in_=w_planes[:].rearrange("p t n -> p n t"))
+            if i == 3:
+                nc.vector.quantize_mx(
+                    out=w_codes[:].bitcast(FP8X4),
+                    scales=w_scales[:],
+                    in_=w_grouped[:].rearrange("p n t -> p (n t)"),
                 )
+            if i == EARLY - 1:
+                merge_early(0, early_calls)
+                merge_early(1, early_high * BN_CALLS)
 
         xt_of = {}
         for g in range(AHEAD):
@@ -186,82 +316,88 @@ def tile_customnetwork_pa_t_kernel(tc, h_lin, gamma, beta, w, b, out):
 
         mean_var = const.tile([P, PACK, 2], F32)
         for e in range(2):
-            nc.vector.bn_aggr(out=mean_var[:, e, :], in_=low_stats[:, early_calls : low_calls + 1, e, :])
+            nc.vector.bn_aggr(out=mean_var[:, e, :], in_=stats[:, 0, early_calls : gpsimd_slot + 1, e, :])
         for e in range(2):
-            nc.vector.tensor_scalar(
-                out=mean_var[:, 2 + e, 0:1], in0=plain_sums[e][:, 0:1], scalar1=1.0 / ROWS, scalar2=None, op0=ALU.mult
-            )
-        off_centre = const.tile([P, 2], F32)
-        nc.vector.tensor_tensor(out=off_centre[:], in0=mean_var[:, 2:4, 0], in1=neg_shift[:], op=ALU.add)
-        off_centre_sq = const.tile([P, 2], F32)
-        nc.vector.tensor_tensor(out=off_centre_sq[:], in0=off_centre[:], in1=off_centre[:], op=ALU.mult)
-        high_square_sum = const.tile([P, 2], F32)
-        nc.vector.tensor_reduce(out=high_square_sum[:], in_=square_sums[:], axis=AXIS.X, op=ALU.add)
-        nc.vector.scalar_tensor_tensor(
-            out=mean_var[:, 2:4, 1],
-            in0=high_square_sum[:],
-            scalar=1.0 / ROWS,
-            in1=off_centre_sq[:],
-            op0=ALU.mult,
-            op1=ALU.subtract,
-        )
+            nc.vector.bn_aggr(out=mean_var[:, 2 + e, :], in_=stats[:, 1, high_late : scalar_slot + 1, e, :])
         std = const.tile([P, PACK], F32)
         nc.scalar.activation(out=std[:], in_=mean_var[:, :, 1], func=FUNC.Sqrt, bias=eps[:], scale=1.0)
+        nc.vector.tensor_tensor(
+            out=gamma_mean[:, 1, :], in0=gamma_mean[:, 0, :], in1=mean_var[:, :, 0], op=ALU.mult
+        )
         inv_std = const.tile([P, PACK], F32)
         nc.vector.reciprocal(out=inv_std[:], in_=std[:])
-        scale_k = const.tile([P, PACK], F32)
-        nc.vector.tensor_tensor(out=scale_k[:], in0=gamma_beta[:, 0, :], in1=inv_std[:], op=ALU.mult)
-        mean_scaled = const.tile([P, PACK], F32)
-        nc.vector.tensor_tensor(out=mean_scaled[:], in0=mean_var[:, :, 0], in1=scale_k[:], op=ALU.mult)
-        offset_k = const.tile([P, PACK], F32)
-        nc.vector.tensor_tensor(out=offset_k[:], in0=gamma_beta[:, 1, :], in1=mean_scaled[:], op=ALU.subtract)
-
-        w_grouped = const.tile([P, N_OUT, PACK], BF16, align_bytes=64)
-        nc.vector.tensor_copy(out=w_grouped[:], in_=w_planes[:].rearrange("p t n -> p n t"))
-        w_codes = const.tile([P, N_OUT], U32, align_bytes=64)
-        w_scales = const.tile([P, N_OUT], U8, align_bytes=64)
-        nc.vector.quantize_mx(
-            out=w_codes[:].bitcast(FP8X4),
-            scales=w_scales[:],
-            in_=w_grouped[:].rearrange("p n t -> p (n t)"),
+        scaled = const.tile([P, 2, PACK], F32)
+        nc.vector.tensor_tensor(
+            out=scaled[:],
+            in0=gamma_mean[:],
+            in1=inv_std[:].unsqueeze(1).to_broadcast([P, 2, PACK]),
+            op=ALU.mult,
         )
+        offset_k = const.tile([P, PACK], F32)
+        nc.vector.tensor_tensor(out=offset_k[:], in0=beta_k[:], in1=scaled[:, 1, :], op=ALU.subtract)
 
+        chunks = [(g, 0, GROUP) for g in range(GROUPS - 1)]
+        chunks.append((GROUPS - 1, 0, GROUP // 2))
+        chunks.append((GROUPS - 1, GROUP // 2, GROUP // 2))
+        last = len(chunks) - 1
         planes_of = {}
         grouped_of = {}
         acc_of = {}
 
-        def normalise(g):
-            planes = stage.tile([P, PACK, GROUP_ROWS], BF16, name="planes")
+        def normalise(s):
+            g, first, count = chunks[s]
+            rows = count * P
+            columns = slice(first * P, first * P + rows)
+            planes = stage.tile([P, PACK, rows], BF16, name="planes")
             for u in range(2):
                 for e in range(2):
                     t = 2 * u + e
-                    nc.scalar.activation(
-                        out=planes[:, t, :],
-                        in_=one_k(xt_of[g][u], e),
-                        func=FUNC.Relu,
-                        bias=offset_k[:, t : t + 1],
-                        scale=scale_k[:, t : t + 1],
-                    )
-            planes_of[g] = planes
+                    scale = scaled[:, 0, t : t + 1]
+                    offset = offset_k[:, t : t + 1]
+                    if s == 0 and u == 1:
+                        nc.vector.tensor_scalar(
+                            out=planes[:, t, :],
+                            in0=one_k(xt_of[g][u], e, columns),
+                            scalar1=scale,
+                            scalar2=offset,
+                            op0=ALU.mult,
+                            op1=ALU.add,
+                        )
+                    else:
+                        nc.scalar.activation(
+                            out=planes[:, t, :],
+                            in_=one_k(xt_of[g][u], e, columns),
+                            func=FUNC.Relu,
+                            bias=offset,
+                            scale=scale,
+                        )
+            planes_of[s] = planes
 
-        def interleave(g):
-            grouped = stage.tile([P, GROUP_ROWS, PACK], BF16, name="grouped", align_bytes=64)
-            nc.vector.tensor_copy(
-                out=grouped[:].rearrange("p (c i) t -> p c t i", i=4),
-                in_=planes_of[g][:].rearrange("p t (c i) -> p c t i", i=4),
-            )
-            grouped_of[g] = grouped
+        def interleave(s):
+            rows = chunks[s][2] * P
+            grouped = stage.tile([P, rows, PACK], BF16, name="grouped", align_bytes=64)
+            target = grouped[:].rearrange("p (c i) t -> p c t i", i=4)
+            source = planes_of[s][:].rearrange("p t (c i) -> p c t i", i=4)
+            if s == 0:
+                nc.vector.tensor_scalar(out=target, in0=source, scalar1=0.0, scalar2=None, op0=ALU.max)
+            elif s == last:
+                nc.scalar.copy(out=target, in_=source)
+            else:
+                nc.vector.tensor_copy(out=target, in_=source)
+            grouped_of[s] = grouped
 
-        def quantise_and_multiply(g):
-            codes = stage.tile([P, GROUP_ROWS], U32, name="codes", align_bytes=64)
-            scales = stage.tile([P, GROUP_ROWS], U8, name="scales", align_bytes=64)
+        def quantise_and_multiply(s):
+            count = chunks[s][2]
+            rows = count * P
+            codes = stage.tile([P, rows], U32, name="codes", align_bytes=64)
+            scales = stage.tile([P, rows], U8, name="scales", align_bytes=64)
             nc.vector.quantize_mx(
                 out=codes[:].bitcast(FP8X4),
                 scales=scales[:],
-                in_=grouped_of[g][:].rearrange("p r t -> p (r t)"),
+                in_=grouped_of[s][:].rearrange("p r t -> p (r t)"),
             )
-            acc = psum_acc.tile([P, GROUP, N_OUT], F32, name="acc")
-            for j in range(GROUP):
+            acc = psum_acc.tile([P, count, N_OUT], F32, name="acc")
+            for j in range(count):
                 block = slice(j * P, (j + 1) * P)
                 nc.tensor.matmul_mx(
                     out=acc[:, j, :],
@@ -272,25 +408,29 @@ def tile_customnetwork_pa_t_kernel(tc, h_lin, gamma, beta, w, b, out):
                     start=True,
                     stop=True,
                 )
-            acc_of[g] = acc
+            acc_of[s] = acc
 
-        def add_bias_and_store(g):
-            result = results.tile([P, GROUP, N_OUT], F32, name="result")
+        def add_bias_and_store(s):
+            g, first, count = chunks[s]
+            result = results.tile([P, count, N_OUT], F32, name="result")
             nc.vector.tensor_tensor(
                 out=result[:],
-                in0=acc_of[g][:],
-                in1=b_rows[:].unsqueeze(1).to_broadcast([P, GROUP, N_OUT]),
+                in0=acc_of[s][:],
+                in1=b_rows[:].unsqueeze(1).to_broadcast([P, count, N_OUT]),
                 op=ALU.add,
             )
-            nc.sync.dma_start(out=out_dram[:, g * GROUP : (g + 1) * GROUP, :], in_=result[:])
+            a0 = g * GROUP + first
+            nc.sync.dma_start(out=out_dram[:, a0 : a0 + count, :], in_=result[:])
 
-        for s in range(GROUPS + 2):
+        for s in range(len(chunks)):
             if s + AHEAD < GROUPS:
                 xt_of[s + AHEAD] = [transpose_half(s + AHEAD, 0), transpose_half(s + AHEAD, 1)]
-            if s < GROUPS:
-                normalise(s)
-                interleave(s)
-            if 1 <= s <= GROUPS:
+            normalise(s)
+            interleave(s)
+            if s >= 1:
                 quantise_and_multiply(s - 1)
             if s >= 2:
                 add_bias_and_store(s - 2)
+        quantise_and_multiply(last)
+        add_bias_and_store(last - 1)
+        add_bias_and_store(last)

@@ -32,13 +32,14 @@ AHEAD = 2
 GPSIMD_GROUPS = (1, 5, 13, 21)
 BANK_GROUPS = [g for g in range(GROUPS) if g not in GPSIMD_GROUPS]
 LAST = BANK_GROUPS[-1]
+SUM_EVERY = 4
 EARLY = 24
 
 
 def owner_of_high(i):
-    if i == len(BANK_GROUPS) - 1 or (i % 4 == 0 and i < EARLY):
-        return "vector"
-    return "scalar_twice" if i % 4 in (2, 3) else "scalar"
+    if i < EARLY:
+        return ("vector", "scalar_twice", "scalar", "scalar")[i % 4]
+    return ("scalar_twice", "vector", "scalar_twice", "vector")[i % 4]
 
 
 VECTOR_HIGH = [i for i in range(len(BANK_GROUPS)) if owner_of_high(i) == "vector"]
@@ -118,8 +119,8 @@ def tile_customnetwork_pa_t_kernel(tc, h_lin, gamma, beta, w, b, out):
 
         low_calls = len(BANK_GROUPS) * BN_CALLS
         early_calls = EARLY * BN_CALLS
-        early_high = len(VECTOR_HIGH) - 1
-        high_late = low_calls - BN_CALLS
+        early_high = len([i for i in VECTOR_HIGH if i < EARLY])
+        high_late = low_calls - BN_CALLS * (len(VECTOR_HIGH) - early_high)
         merged, gpsimd_slot, scalar_slot = low_calls, low_calls + 1, low_calls + 2
         stats = const.tile([P, 2, low_calls + 3, 2, 3], F32)
         early_rows = (EARLY * GROUP_ROWS, early_high * GROUP_ROWS)
@@ -234,11 +235,12 @@ def tile_customnetwork_pa_t_kernel(tc, h_lin, gamma, beta, w, b, out):
                 out=stats[:, 1, scalar_slot, :, 2], in0=spread[:], scalar1=0.0, scalar2=None, op0=ALU.max
             )
 
+        waiting_sums = []
         for g in range(GROUPS):
             if g in GPSIMD_GROUPS:
                 squares_on_gpsimd(g)
                 for t in range(PACK):
-                    column_sum(gpsimd_bank, GPSIMD_GROUPS.index(g) * PACK + t, g, t)
+                    waiting_sums.append((gpsimd_bank, GPSIMD_GROUPS.index(g) * PACK + t, g, t))
                 continue
             i = BANK_GROUPS.index(g)
             owner = owner_of_high(i)
@@ -261,7 +263,7 @@ def tile_customnetwork_pa_t_kernel(tc, h_lin, gamma, beta, w, b, out):
             bn_bank(xt_low, 0, i * BN_CALLS)
             if owner == "vector":
                 v = VECTOR_HIGH.index(i)
-                bn_bank(xt_high, 1, high_late if g == LAST else v * BN_CALLS)
+                bn_bank(xt_high, 1, v * BN_CALLS if i < EARLY else high_late + (v - early_high) * BN_CALLS)
                 if i == 0:
                     nc.vector.tensor_scalar(
                         out=neg_shift[:], in0=stats[:, 1, 0, :, 1], scalar1=-1.0, scalar2=None, op0=ALU.mult
@@ -288,7 +290,11 @@ def tile_customnetwork_pa_t_kernel(tc, h_lin, gamma, beta, w, b, out):
                             accum_out=twice_sums[:, e, d : d + 1],
                         )
                     else:
-                        column_sum(once_bank, ONCE_HIGH.index(i) * 2 + e, g, 2 + e)
+                        waiting_sums.append((once_bank, ONCE_HIGH.index(i) * 2 + e, g, 2 + e))
+            if i % SUM_EVERY == SUM_EVERY - 1:
+                for bank, column, rows_of, t in waiting_sums:
+                    column_sum(bank, column, rows_of, t)
+                waiting_sums.clear()
             if i == 2:
                 gb_t = psum_x.tile([P, GROUP_ROWS], F32, name="xt")
                 for u in range(2):

@@ -154,12 +154,11 @@ def tile_customnetwork_pa_t_kernel(tc, h_lin, gamma, beta, w, b, out):
         def merge_early(u, calls):
             for e in range(2):
                 nc.vector.bn_aggr(out=stats[:, u, merged, e, 1:3], in_=stats[:, u, 0:calls, e, :])
-            nc.vector.tensor_scalar(
+            nc.scalar.activation(
                 out=stats[:, u, merged, :, 2],
-                in0=stats[:, u, merged, :, 2],
-                scalar1=float(early_rows[u]),
-                scalar2=None,
-                op0=ALU.mult,
+                in_=stats[:, u, merged, :, 2],
+                func=FUNC.Copy,
+                scale=float(early_rows[u]),
             )
 
         def squares_on_gpsimd(g):
@@ -265,8 +264,8 @@ def tile_customnetwork_pa_t_kernel(tc, h_lin, gamma, beta, w, b, out):
                 v = VECTOR_HIGH.index(i)
                 bn_bank(xt_high, 1, v * BN_CALLS if i < EARLY else high_late + (v - early_high) * BN_CALLS)
                 if i == 0:
-                    nc.vector.tensor_scalar(
-                        out=neg_shift[:], in0=stats[:, 1, 0, :, 1], scalar1=-1.0, scalar2=None, op0=ALU.mult
+                    nc.scalar.activation(
+                        out=neg_shift[:], in_=stats[:, 1, 0, :, 1], func=FUNC.Copy, scale=-1.0
                     )
             else:
                 s = SCALAR_HIGH.index(i)
@@ -305,13 +304,7 @@ def tile_customnetwork_pa_t_kernel(tc, h_lin, gamma, beta, w, b, out):
                     pairs = gb_t[:].bitcast(BF16)[:, 2 * u * P : 2 * u * P + 4]
                     nc.vector.tensor_copy(out=gamma_mean[:, 0, 2 * u : 2 * u + 2], in_=pairs[:, 0:2])
                     nc.vector.tensor_copy(out=beta_k[:, 2 * u : 2 * u + 2], in_=pairs[:, 2:4])
-                nc.vector.tensor_copy(out=w_grouped[:], in_=w_planes[:].rearrange("p t n -> p n t"))
-            if i == 3:
-                nc.vector.quantize_mx(
-                    out=w_codes[:].bitcast(FP8X4),
-                    scales=w_scales[:],
-                    in_=w_grouped[:].rearrange("p n t -> p (n t)"),
-                )
+                nc.scalar.copy(out=w_grouped[:], in_=w_planes[:].rearrange("p t n -> p n t"))
             if i == EARLY - 1:
                 merge_early(0, early_calls)
                 merge_early(1, early_high * BN_CALLS)
@@ -433,6 +426,12 @@ def tile_customnetwork_pa_t_kernel(tc, h_lin, gamma, beta, w, b, out):
                 xt_of[s + AHEAD] = [transpose_half(s + AHEAD, 0), transpose_half(s + AHEAD, 1)]
             normalise(s)
             interleave(s)
+            if s == 0:
+                nc.vector.quantize_mx(
+                    out=w_codes[:].bitcast(FP8X4),
+                    scales=w_scales[:],
+                    in_=w_grouped[:].rearrange("p n t -> p (n t)"),
+                )
             if s >= 1:
                 quantise_and_multiply(s - 1)
             if s >= 2:

@@ -32,14 +32,15 @@ AHEAD = 2
 GPSIMD_GROUPS = (1, 5, 13, 21)
 BANK_GROUPS = [g for g in range(GROUPS) if g not in GPSIMD_GROUPS]
 LAST = BANK_GROUPS[-1]
+SCALAR_INTERLEAVES = (GROUPS - 1, GROUPS)
 SUM_EVERY = 4
 EARLY = 24
 
 
 def owner_of_high(i):
-    if i < EARLY:
-        return ("vector", "scalar_twice", "scalar", "scalar")[i % 4]
-    return ("scalar_twice", "vector", "scalar_twice", "vector")[i % 4]
+    if i % 5 == 4:
+        return "vector"
+    return "scalar_twice" if i % 5 == 1 and i < EARLY or i % 5 == 3 and i < 20 else "scalar"
 
 
 VECTOR_HIGH = [i for i in range(len(BANK_GROUPS)) if owner_of_high(i) == "vector"]
@@ -123,6 +124,7 @@ def tile_customnetwork_pa_t_kernel(tc, h_lin, gamma, beta, w, b, out):
         high_late = low_calls - BN_CALLS * (len(VECTOR_HIGH) - early_high)
         merged, gpsimd_slot, scalar_slot = low_calls, low_calls + 1, low_calls + 2
         stats = const.tile([P, 2, low_calls + 3, 2, 3], F32)
+        early_once = len([i for i in ONCE_HIGH if i < EARLY])
         early_rows = (EARLY * GROUP_ROWS, early_high * GROUP_ROWS)
         gpsimd_rows = len(GPSIMD_GROUPS) * GROUP_ROWS
         scalar_rows = len(SCALAR_HIGH) * GROUP_ROWS
@@ -131,6 +133,7 @@ def tile_customnetwork_pa_t_kernel(tc, h_lin, gamma, beta, w, b, out):
         nc.vector.memset(stats[:, :, gpsimd_slot, :, :], float(gpsimd_rows))
         nc.vector.memset(stats[:, 1, scalar_slot, :, :], float(scalar_rows))
 
+        shift_stats = const.tile([P, 2, 3], F32)
         neg_shift = const.tile([P, 2], F32)
         square_sums = const.tile([P, 2, len(SCALAR_HIGH)], F32)
         twice_sums = const.tile([P, 2, len(TWICE_HIGH)], F32)
@@ -204,35 +207,48 @@ def tile_customnetwork_pa_t_kernel(tc, h_lin, gamma, beta, w, b, out):
                 out=stats[:, :, gpsimd_slot, :, 2], in0=spread[:], scalar1=0.0, scalar2=None, op0=ALU.max
             )
 
-        def close_scalar():
-            once = const.tile([P, 2], F32, name="s_once")
+        def once_sums(first, end, name):
+            total = const.tile([P, 2], F32, name=name)
             nc.vector.tensor_reduce(
-                out=once[:],
-                in_=once_bank[:, 0 : len(ONCE_HIGH) * 2 * ONES].rearrange(
-                    "p (i e o) -> p e i o", e=2, o=ONES
-                )[:, :, :, 0],
+                out=total[:],
+                in_=once_bank[:, first * 2 * ONES : end * 2 * ONES].rearrange("p (i e o) -> p e i o", e=2, o=ONES)[
+                    :, :, :, 0
+                ],
                 axis=AXIS.X,
                 op=ALU.add,
             )
+            return total
+
+        def open_scalar():
+            once = once_sums(0, early_once, "s_once")
             twice = const.tile([P, 2], F32, name="s_twice")
             nc.vector.tensor_reduce(out=twice[:], in_=twice_sums[:], axis=AXIS.X, op=ALU.add)
-            squares = const.tile([P, 2], F32, name="s_squares")
-            nc.vector.tensor_reduce(out=squares[:], in_=square_sums[:], axis=AXIS.X, op=ALU.add)
             sums = const.tile([P, 2], F32, name="s_sums")
             nc.vector.tensor_tensor(out=sums[:], in0=once[:], in1=twice[:], op=ALU.add)
-            mean = stats[:, 1, scalar_slot, :, 1]
-            nc.vector.tensor_scalar(out=mean, in0=sums[:], scalar1=1.0 / scalar_rows, scalar2=None, op0=ALU.mult)
+            share = const.tile([P, 2], F32, name="s_share")
+            nc.vector.tensor_scalar(out=share[:], in0=sums[:], scalar1=1.0 / scalar_rows, scalar2=None, op0=ALU.mult)
+            off_share = const.tile([P, 2], F32, name="s_off_share")
+            nc.vector.tensor_tensor(out=off_share[:], in0=share[:], in1=neg_shift[:], op=ALU.add)
+            return share, off_share
+
+        def close_scalar(share, off_share):
+            late = once_sums(early_once, len(ONCE_HIGH), "s_late")
             off = const.tile([P, 2], F32, name="s_off")
-            nc.vector.tensor_tensor(out=off[:], in0=mean, in1=neg_shift[:], op=ALU.add)
+            for total, early in ((off[:], off_share), (stats[:, 1, scalar_slot, :, 1], share)):
+                nc.vector.scalar_tensor_tensor(
+                    out=total, in0=late[:], scalar=1.0 / scalar_rows, in1=early[:], op0=ALU.mult, op1=ALU.add
+                )
+            squares = const.tile([P, 2], F32, name="s_squares")
+            nc.vector.tensor_reduce(
+                out=squares[:], in_=square_sums[:, :, 0 : len(SCALAR_HIGH) - 1], axis=AXIS.X, op=ALU.add
+            )
             off_sq = const.tile([P, 2], F32, name="s_off_sq")
             nc.vector.tensor_tensor(out=off_sq[:], in0=off[:], in1=off[:], op=ALU.mult)
             spread = const.tile([P, 2], F32, name="s_spread")
             nc.vector.scalar_tensor_tensor(
                 out=spread[:], in0=off_sq[:], scalar=-float(scalar_rows), in1=squares[:], op0=ALU.mult, op1=ALU.add
             )
-            nc.vector.tensor_scalar(
-                out=stats[:, 1, scalar_slot, :, 2], in0=spread[:], scalar1=0.0, scalar2=None, op0=ALU.max
-            )
+            return spread
 
         waiting_sums = []
         for g in range(GROUPS):
@@ -254,19 +270,20 @@ def tile_customnetwork_pa_t_kernel(tc, h_lin, gamma, beta, w, b, out):
                         start=True,
                         stop=True,
                     )
-            xt_low = transpose_half(g, 0)
-            xt_high = transpose_half(g, 1)
-            if g == LAST:
-                close_scalar()
-                close_gpsimd()
+            if i == 0:
+                xt_high = transpose_half(g, 1)
+                nc.vector.bn_stats(
+                    out=shift_stats[:].rearrange("p e s -> p (e s)"), in_=xt_high[:].bitcast(BF16)[:, 0 : 2 * P]
+                )
+                nc.scalar.activation(out=neg_shift[:], in_=shift_stats[:, :, 1], func=FUNC.Copy, scale=-1.0)
+                xt_low = transpose_half(g, 0)
+            else:
+                xt_low = transpose_half(g, 0)
+                xt_high = transpose_half(g, 1)
             bn_bank(xt_low, 0, i * BN_CALLS)
             if owner == "vector":
                 v = VECTOR_HIGH.index(i)
                 bn_bank(xt_high, 1, v * BN_CALLS if i < EARLY else high_late + (v - early_high) * BN_CALLS)
-                if i == 0:
-                    nc.scalar.activation(
-                        out=neg_shift[:], in_=stats[:, 1, 0, :, 1], func=FUNC.Copy, scale=-1.0
-                    )
             else:
                 s = SCALAR_HIGH.index(i)
                 for e in range(2):
@@ -290,7 +307,7 @@ def tile_customnetwork_pa_t_kernel(tc, h_lin, gamma, beta, w, b, out):
                         )
                     else:
                         waiting_sums.append((once_bank, ONCE_HIGH.index(i) * 2 + e, g, 2 + e))
-            if i % SUM_EVERY == SUM_EVERY - 1:
+            if i % SUM_EVERY == SUM_EVERY - 1 or i > EARLY:
                 for bank, column, rows_of, t in waiting_sums:
                     column_sum(bank, column, rows_of, t)
                 waiting_sums.clear()
@@ -308,14 +325,24 @@ def tile_customnetwork_pa_t_kernel(tc, h_lin, gamma, beta, w, b, out):
             if i == EARLY - 1:
                 merge_early(0, early_calls)
                 merge_early(1, early_high * BN_CALLS)
+            if i == EARLY:
+                share, off_share = open_scalar()
 
         xt_of = {}
         for g in range(AHEAD):
             xt_of[g] = [transpose_half(g, 0), transpose_half(g, 1)]
 
         mean_var = const.tile([P, PACK, 2], F32)
+        close_gpsimd()
         for e in range(2):
             nc.vector.bn_aggr(out=mean_var[:, e, :], in_=stats[:, 0, early_calls : gpsimd_slot + 1, e, :])
+        spread = close_scalar(share, off_share)
+        nc.vector.tensor_tensor(
+            out=stats[:, 1, scalar_slot, :, 2],
+            in0=spread[:],
+            in1=square_sums[:, :, len(SCALAR_HIGH) - 1],
+            op=ALU.add,
+        )
         for e in range(2):
             nc.vector.bn_aggr(out=mean_var[:, 2 + e, :], in_=stats[:, 1, high_late : scalar_slot + 1, e, :])
         std = const.tile([P, PACK], F32)
@@ -379,7 +406,7 @@ def tile_customnetwork_pa_t_kernel(tc, h_lin, gamma, beta, w, b, out):
             source = planes_of[s][:].rearrange("p t (c i) -> p c t i", i=4)
             if s == 0:
                 nc.vector.tensor_scalar(out=target, in0=source, scalar1=0.0, scalar2=None, op0=ALU.max)
-            elif s == last:
+            elif s in SCALAR_INTERLEAVES:
                 nc.scalar.copy(out=target, in_=source)
             else:
                 nc.vector.tensor_copy(out=target, in_=source)

@@ -32,7 +32,7 @@ AHEAD = 2
 GPSIMD_GROUPS = (1, 5, 13, 21)
 BANK_GROUPS = [g for g in range(GROUPS) if g not in GPSIMD_GROUPS]
 LAST = BANK_GROUPS[-1]
-SCALAR_INTERLEAVES = (GROUPS - 1, GROUPS)
+SCALAR_INTERLEAVES = (GROUPS, GROUPS + 1)
 SUM_EVERY = 4
 EARLY = 24
 
@@ -60,7 +60,7 @@ def tile_customnetwork_pa_t_kernel(tc, h_lin, gamma, beta, w, b, out):
         const = stack.enter_context(tc.tile_pool(name="const", bufs=1))
         resident = stack.enter_context(tc.tile_pool(name="resident", bufs=GROUPS))
         unread = stack.enter_context(tc.tile_pool(name="unread", bufs=4))
-        stage = stack.enter_context(tc.tile_pool(name="stage", bufs=3))
+        stage = stack.enter_context(tc.tile_pool(name="stage", bufs=4))
         results = stack.enter_context(tc.tile_pool(name="results", bufs=4))
         psum_x = stack.enter_context(tc.psum_pool(name="psum_x", bufs=6))
         psum_acc = stack.enter_context(tc.psum_pool(name="psum_acc", bufs=2))
@@ -82,7 +82,7 @@ def tile_customnetwork_pa_t_kernel(tc, h_lin, gamma, beta, w, b, out):
         w_planes = const.tile([P, PACK, N_OUT], BF16)
         nc.scalar.dma_start(out=w_planes[:], in_=w.rearrange("(p t) n -> p t n", t=PACK))
         warm = const.tile([P, 1], F32)
-        nc.scalar.activation(out=warm[:], in_=eps[:], func=FUNC.Sqrt)
+        nc.scalar.activation(out=warm[:], in_=eps[:], func=FUNC.Abs_reciprocal_sqrt)
 
         x_tiles = []
         for g in range(GROUPS):
@@ -125,6 +125,7 @@ def tile_customnetwork_pa_t_kernel(tc, h_lin, gamma, beta, w, b, out):
         merged, gpsimd_slot, scalar_slot = low_calls, low_calls + 1, low_calls + 2
         stats = const.tile([P, 2, low_calls + 3, 2, 3], F32)
         early_once = len([i for i in ONCE_HIGH if i < EARLY])
+        late_column = (len(GPSIMD_GROUPS) + 1) * PACK
         early_rows = (EARLY * GROUP_ROWS, early_high * GROUP_ROWS)
         gpsimd_rows = len(GPSIMD_GROUPS) * GROUP_ROWS
         scalar_rows = len(SCALAR_HIGH) * GROUP_ROWS
@@ -179,48 +180,20 @@ def tile_customnetwork_pa_t_kernel(tc, h_lin, gamma, beta, w, b, out):
                         op=ALU.add,
                     )
 
-        def close_gpsimd():
-            sums = const.tile([P, 2, 2], F32, name="g_sums")
-            nc.vector.tensor_reduce(
-                out=sums[:],
-                in_=gpsimd_bank[:, 0 : len(GPSIMD_GROUPS) * PACK * ONES].rearrange(
-                    "p (g u e o) -> p u e g o", u=2, e=2, o=ONES
-                )[:, :, :, :, 0],
-                axis=AXIS.X,
-                op=ALU.add,
-            )
-            mean = stats[:, :, gpsimd_slot, :, 1]
-            nc.vector.tensor_scalar(out=mean, in0=sums[:], scalar1=1.0 / gpsimd_rows, scalar2=None, op0=ALU.mult)
-            mean_sums = const.tile([P, 2, 2], F32, name="g_mean_sums")
-            nc.vector.tensor_tensor(out=mean_sums[:], in0=mean, in1=sums[:], op=ALU.mult)
-            spread = const.tile([P, 2, 2], F32, name="g_spread")
-            base = len(GPSIMD_GROUPS) * PACK
-            nc.vector.tensor_tensor(
-                out=spread[:],
-                in0=gpsimd_bank[:, base * ONES : (base + PACK) * ONES].rearrange(
-                    "p (u e o) -> p u e o", u=2, o=ONES
-                )[:, :, :, 0],
-                in1=mean_sums[:],
-                op=ALU.subtract,
-            )
-            nc.vector.tensor_scalar(
-                out=stats[:, :, gpsimd_slot, :, 2], in0=spread[:], scalar1=0.0, scalar2=None, op0=ALU.max
-            )
-
-        def once_sums(first, end, name):
+        def once_sums(bank, column, count, name):
             total = const.tile([P, 2], F32, name=name)
             nc.vector.tensor_reduce(
                 out=total[:],
-                in_=once_bank[:, first * 2 * ONES : end * 2 * ONES].rearrange("p (i e o) -> p e i o", e=2, o=ONES)[
-                    :, :, :, 0
-                ],
+                in_=bank[:, column * ONES : (column + 2 * count) * ONES].rearrange(
+                    "p (i e o) -> p e i o", e=2, o=ONES
+                )[:, :, :, 0],
                 axis=AXIS.X,
                 op=ALU.add,
             )
             return total
 
         def open_scalar():
-            once = once_sums(0, early_once, "s_once")
+            once = once_sums(once_bank, 0, early_once, "s_once")
             twice = const.tile([P, 2], F32, name="s_twice")
             nc.vector.tensor_reduce(out=twice[:], in_=twice_sums[:], axis=AXIS.X, op=ALU.add)
             sums = const.tile([P, 2], F32, name="s_sums")
@@ -231,24 +204,51 @@ def tile_customnetwork_pa_t_kernel(tc, h_lin, gamma, beta, w, b, out):
             nc.vector.tensor_tensor(out=off_share[:], in0=share[:], in1=neg_shift[:], op=ALU.add)
             return share, off_share
 
-        def close_scalar(share, off_share):
-            late = once_sums(early_once, len(ONCE_HIGH), "s_late")
-            off = const.tile([P, 2], F32, name="s_off")
+        def close_gpsimd_and_scalar(share, off_share):
+            base = len(GPSIMD_GROUPS) * PACK * ONES
+            g_mean = stats[:, :, gpsimd_slot, :, 1]
+            late = once_sums(gpsimd_bank, late_column, len(ONCE_HIGH) - early_once, "s_late")
+            g_sums = const.tile([P, 2, 2], F32)
+            nc.vector.tensor_reduce(
+                out=g_sums[:],
+                in_=gpsimd_bank[:, 0:base].rearrange("p (g u e o) -> p u e g o", u=2, e=2, o=ONES)[:, :, :, :, 0],
+                axis=AXIS.X,
+                op=ALU.add,
+            )
+            off = const.tile([P, 2], F32)
             for total, early in ((off[:], off_share), (stats[:, 1, scalar_slot, :, 1], share)):
                 nc.vector.scalar_tensor_tensor(
                     out=total, in0=late[:], scalar=1.0 / scalar_rows, in1=early[:], op0=ALU.mult, op1=ALU.add
                 )
+            nc.vector.tensor_scalar(out=g_mean, in0=g_sums[:], scalar1=1.0 / gpsimd_rows, scalar2=None, op0=ALU.mult)
+            off_sq = const.tile([P, 2], F32)
+            nc.vector.tensor_tensor(out=off_sq[:], in0=off[:], in1=off[:], op=ALU.mult)
             squares = const.tile([P, 2], F32, name="s_squares")
             nc.vector.tensor_reduce(
                 out=squares[:], in_=square_sums[:, :, 0 : len(SCALAR_HIGH) - 1], axis=AXIS.X, op=ALU.add
             )
-            off_sq = const.tile([P, 2], F32, name="s_off_sq")
-            nc.vector.tensor_tensor(out=off_sq[:], in0=off[:], in1=off[:], op=ALU.mult)
-            spread = const.tile([P, 2], F32, name="s_spread")
+            g_mean_sums = const.tile([P, 2, 2], F32)
+            nc.vector.tensor_tensor(out=g_mean_sums[:], in0=g_mean, in1=g_sums[:], op=ALU.mult)
+            spread = const.tile([P, 2], F32)
             nc.vector.scalar_tensor_tensor(
                 out=spread[:], in0=off_sq[:], scalar=-float(scalar_rows), in1=squares[:], op0=ALU.mult, op1=ALU.add
             )
-            return spread
+            g_spread = const.tile([P, 2, 2], F32)
+            nc.vector.tensor_tensor(
+                out=g_spread[:],
+                in0=gpsimd_bank[:, base : base + PACK * ONES].rearrange("p (u e o) -> p u e o", u=2, o=ONES)[:, :, :, 0],
+                in1=g_mean_sums[:],
+                op=ALU.subtract,
+            )
+            nc.vector.tensor_tensor(
+                out=stats[:, 1, scalar_slot, :, 2],
+                in0=spread[:],
+                in1=square_sums[:, :, len(SCALAR_HIGH) - 1],
+                op=ALU.add,
+            )
+            nc.vector.tensor_scalar(
+                out=stats[:, :, gpsimd_slot, :, 2], in0=g_spread[:], scalar1=0.0, scalar2=None, op0=ALU.max
+            )
 
         waiting_sums = []
         for g in range(GROUPS):
@@ -306,7 +306,11 @@ def tile_customnetwork_pa_t_kernel(tc, h_lin, gamma, beta, w, b, out):
                             accum_out=twice_sums[:, e, d : d + 1],
                         )
                     else:
-                        waiting_sums.append((once_bank, ONCE_HIGH.index(i) * 2 + e, g, 2 + e))
+                        o = ONCE_HIGH.index(i)
+                        if o < early_once:
+                            waiting_sums.append((once_bank, o * 2 + e, g, 2 + e))
+                        else:
+                            waiting_sums.append((gpsimd_bank, late_column + (o - early_once) * 2 + e, g, 2 + e))
             if i % SUM_EVERY == SUM_EVERY - 1 or i > EARLY:
                 for bank, column, rows_of, t in waiting_sums:
                     column_sum(bank, column, rows_of, t)
@@ -333,25 +337,18 @@ def tile_customnetwork_pa_t_kernel(tc, h_lin, gamma, beta, w, b, out):
             xt_of[g] = [transpose_half(g, 0), transpose_half(g, 1)]
 
         mean_var = const.tile([P, PACK, 2], F32)
-        close_gpsimd()
-        for e in range(2):
-            nc.vector.bn_aggr(out=mean_var[:, e, :], in_=stats[:, 0, early_calls : gpsimd_slot + 1, e, :])
-        spread = close_scalar(share, off_share)
-        nc.vector.tensor_tensor(
-            out=stats[:, 1, scalar_slot, :, 2],
-            in0=spread[:],
-            in1=square_sums[:, :, len(SCALAR_HIGH) - 1],
-            op=ALU.add,
-        )
+        close_gpsimd_and_scalar(share, off_share)
         for e in range(2):
             nc.vector.bn_aggr(out=mean_var[:, 2 + e, :], in_=stats[:, 1, high_late : scalar_slot + 1, e, :])
-        std = const.tile([P, PACK], F32)
-        nc.scalar.activation(out=std[:], in_=mean_var[:, :, 1], func=FUNC.Sqrt, bias=eps[:], scale=1.0)
+        for e in range(2):
+            nc.vector.bn_aggr(out=mean_var[:, e, :], in_=stats[:, 0, early_calls : gpsimd_slot + 1, e, :])
+        inv_std = const.tile([P, PACK], F32)
+        nc.scalar.activation(
+            out=inv_std[:], in_=mean_var[:, :, 1], func=FUNC.Abs_reciprocal_sqrt, bias=eps[:], scale=1.0
+        )
         nc.vector.tensor_tensor(
             out=gamma_mean[:, 1, :], in0=gamma_mean[:, 0, :], in1=mean_var[:, :, 0], op=ALU.mult
         )
-        inv_std = const.tile([P, PACK], F32)
-        nc.vector.reciprocal(out=inv_std[:], in_=std[:])
         scaled = const.tile([P, 2, PACK], F32)
         nc.vector.tensor_tensor(
             out=scaled[:],
@@ -362,9 +359,10 @@ def tile_customnetwork_pa_t_kernel(tc, h_lin, gamma, beta, w, b, out):
         offset_k = const.tile([P, PACK], F32)
         nc.vector.tensor_tensor(out=offset_k[:], in0=beta_k[:], in1=scaled[:, 1, :], op=ALU.subtract)
 
-        chunks = [(g, 0, GROUP) for g in range(GROUPS - 1)]
-        chunks.append((GROUPS - 1, 0, GROUP // 2))
-        chunks.append((GROUPS - 1, GROUP // 2, GROUP // 2))
+        halves = [(0, GROUP // 2), (GROUP // 2, GROUP // 2)]
+        chunks = [(0, *half) for half in halves]
+        chunks += [(g, 0, GROUP) for g in range(1, GROUPS - 1)]
+        chunks += [(GROUPS - 1, *half) for half in halves]
         last = len(chunks) - 1
         planes_of = {}
         grouped_of = {}
@@ -380,7 +378,7 @@ def tile_customnetwork_pa_t_kernel(tc, h_lin, gamma, beta, w, b, out):
                     t = 2 * u + e
                     scale = scaled[:, 0, t : t + 1]
                     offset = offset_k[:, t : t + 1]
-                    if s == 0 and u == 1:
+                    if g == 0 and u == 1:
                         nc.vector.tensor_scalar(
                             out=planes[:, t, :],
                             in0=one_k(xt_of[g][u], e, columns),
@@ -404,7 +402,7 @@ def tile_customnetwork_pa_t_kernel(tc, h_lin, gamma, beta, w, b, out):
             grouped = stage.tile([P, rows, PACK], BF16, name="grouped", align_bytes=64)
             target = grouped[:].rearrange("p (c i) t -> p c t i", i=4)
             source = planes_of[s][:].rearrange("p t (c i) -> p c t i", i=4)
-            if s == 0:
+            if chunks[s][0] == 0:
                 nc.vector.tensor_scalar(out=target, in0=source, scalar1=0.0, scalar2=None, op0=ALU.max)
             elif s in SCALAR_INTERLEAVES:
                 nc.scalar.copy(out=target, in_=source)
@@ -449,8 +447,9 @@ def tile_customnetwork_pa_t_kernel(tc, h_lin, gamma, beta, w, b, out):
             nc.sync.dma_start(out=out_dram[:, a0 : a0 + count, :], in_=result[:])
 
         for s in range(len(chunks)):
-            if s + AHEAD < GROUPS:
-                xt_of[s + AHEAD] = [transpose_half(s + AHEAD, 0), transpose_half(s + AHEAD, 1)]
+            g, first, count = chunks[s]
+            if first == 0 and g + AHEAD < GROUPS:
+                xt_of[g + AHEAD] = [transpose_half(g + AHEAD, 0), transpose_half(g + AHEAD, 1)]
             normalise(s)
             interleave(s)
             if s == 0:

@@ -137,6 +137,7 @@ def tile_customnetwork_pa_t_kernel(tc, h_lin, gamma, beta, w, b, out):
         shift_stats = const.tile([P, 2, 3], F32)
         neg_shift = const.tile([P, 2], F32)
         square_sums = const.tile([P, 2, len(SCALAR_HIGH)], F32)
+        sum_parts = const.tile([P, 2, 3], F32)
         twice_sums = const.tile([P, 2, len(TWICE_HIGH)], F32)
         once_bank = psum_acc.tile([P, GROUP_ROWS], F32, name="acc")
         gpsimd_bank = psum_acc.tile([P, GROUP_ROWS], F32, name="acc")
@@ -180,34 +181,20 @@ def tile_customnetwork_pa_t_kernel(tc, h_lin, gamma, beta, w, b, out):
                         op=ALU.add,
                     )
 
-        def once_sums(bank, column, count, name):
-            total = const.tile([P, 2], F32, name=name)
+        def sum_columns(bank, column, count, part):
             nc.vector.tensor_reduce(
-                out=total[:],
+                out=sum_parts[:, :, part],
                 in_=bank[:, column * ONES : (column + 2 * count) * ONES].rearrange(
                     "p (i e o) -> p e i o", e=2, o=ONES
                 )[:, :, :, 0],
                 axis=AXIS.X,
                 op=ALU.add,
             )
-            return total
 
-        def open_scalar():
-            once = once_sums(once_bank, 0, early_once, "s_once")
-            twice = const.tile([P, 2], F32, name="s_twice")
-            nc.vector.tensor_reduce(out=twice[:], in_=twice_sums[:], axis=AXIS.X, op=ALU.add)
-            sums = const.tile([P, 2], F32, name="s_sums")
-            nc.vector.tensor_tensor(out=sums[:], in0=once[:], in1=twice[:], op=ALU.add)
-            share = const.tile([P, 2], F32, name="s_share")
-            nc.vector.tensor_scalar(out=share[:], in0=sums[:], scalar1=1.0 / scalar_rows, scalar2=None, op0=ALU.mult)
-            off_share = const.tile([P, 2], F32, name="s_off_share")
-            nc.vector.tensor_tensor(out=off_share[:], in0=share[:], in1=neg_shift[:], op=ALU.add)
-            return share, off_share
-
-        def close_gpsimd_and_scalar(share, off_share):
+        def close_gpsimd_and_scalar():
             base = len(GPSIMD_GROUPS) * PACK * ONES
             g_mean = stats[:, :, gpsimd_slot, :, 1]
-            late = once_sums(gpsimd_bank, late_column, len(ONCE_HIGH) - early_once, "s_late")
+            sum_columns(gpsimd_bank, late_column, len(ONCE_HIGH) - early_once, 2)
             g_sums = const.tile([P, 2, 2], F32)
             nc.vector.tensor_reduce(
                 out=g_sums[:],
@@ -215,12 +202,16 @@ def tile_customnetwork_pa_t_kernel(tc, h_lin, gamma, beta, w, b, out):
                 axis=AXIS.X,
                 op=ALU.add,
             )
-            off = const.tile([P, 2], F32)
-            for total, early in ((off[:], off_share), (stats[:, 1, scalar_slot, :, 1], share)):
-                nc.vector.scalar_tensor_tensor(
-                    out=total, in0=late[:], scalar=1.0 / scalar_rows, in1=early[:], op0=ALU.mult, op1=ALU.add
-                )
+            sums = const.tile([P, 2], F32, name="s_sums")
+            nc.vector.tensor_reduce(out=sums[:], in_=sum_parts[:], axis=AXIS.X, op=ALU.add)
             nc.vector.tensor_scalar(out=g_mean, in0=g_sums[:], scalar1=1.0 / gpsimd_rows, scalar2=None, op0=ALU.mult)
+            off = const.tile([P, 2], F32)
+            nc.vector.scalar_tensor_tensor(
+                out=off[:], in0=sums[:], scalar=1.0 / scalar_rows, in1=neg_shift[:], op0=ALU.mult, op1=ALU.add
+            )
+            nc.vector.tensor_scalar(
+                out=stats[:, 1, scalar_slot, :, 1], in0=sums[:], scalar1=1.0 / scalar_rows, scalar2=None, op0=ALU.mult
+            )
             off_sq = const.tile([P, 2], F32)
             nc.vector.tensor_tensor(out=off_sq[:], in0=off[:], in1=off[:], op=ALU.mult)
             squares = const.tile([P, 2], F32, name="s_squares")
@@ -330,14 +321,15 @@ def tile_customnetwork_pa_t_kernel(tc, h_lin, gamma, beta, w, b, out):
                 merge_early(0, early_calls)
                 merge_early(1, early_high * BN_CALLS)
             if i == EARLY:
-                share, off_share = open_scalar()
+                sum_columns(once_bank, 0, early_once, 0)
+                nc.vector.tensor_reduce(out=sum_parts[:, :, 1], in_=twice_sums[:], axis=AXIS.X, op=ALU.add)
 
         xt_of = {}
         for g in range(AHEAD):
             xt_of[g] = [transpose_half(g, 0), transpose_half(g, 1)]
 
         mean_var = const.tile([P, PACK, 2], F32)
-        close_gpsimd_and_scalar(share, off_share)
+        close_gpsimd_and_scalar()
         for e in range(2):
             nc.vector.bn_aggr(out=mean_var[:, 2 + e, :], in_=stats[:, 1, high_late : scalar_slot + 1, e, :])
         for e in range(2):

@@ -70,8 +70,6 @@ def tile_customnetwork_pa_t_kernel(tc, h_lin, gamma, beta, w, b, out):
         nc.vector.memset(eps[:], BN_EPS)
         ones = const.tile([P, ONES], BF16)
         nc.vector.memset(ones[:], 1.0)
-        ones_f32 = const.tile([P, ONES], F32)
-        nc.vector.memset(ones_f32[:], 1.0)
         gb_rows = const.tile([P, K], BF16)
         nc.vector.memset(gb_rows[:], 0.0)
         ident = const.tile([P, P], F32)
@@ -123,9 +121,9 @@ def tile_customnetwork_pa_t_kernel(tc, h_lin, gamma, beta, w, b, out):
         early_high = len([i for i in VECTOR_HIGH if i < EARLY])
         high_late = low_calls - BN_CALLS * (len(VECTOR_HIGH) - early_high)
         merged, gpsimd_slot, scalar_slot = low_calls, low_calls + 1, low_calls + 2
-        stats = const.tile([P, 2, low_calls + 3, 2, 3], F32)
+        stats = const.tile([P, 2, low_calls + 4, 2, 3], F32)
         early_once = len([i for i in ONCE_HIGH if i < EARLY])
-        late_column = (len(GPSIMD_GROUPS) + 1) * PACK
+        gpsimd_column = early_once * 2
         early_rows = (EARLY * GROUP_ROWS, early_high * GROUP_ROWS)
         gpsimd_rows = len(GPSIMD_GROUPS) * GROUP_ROWS
         scalar_rows = len(SCALAR_HIGH) * GROUP_ROWS
@@ -137,10 +135,9 @@ def tile_customnetwork_pa_t_kernel(tc, h_lin, gamma, beta, w, b, out):
         shift_stats = const.tile([P, 2, 3], F32)
         neg_shift = const.tile([P, 2], F32)
         square_sums = const.tile([P, 2, len(SCALAR_HIGH)], F32)
-        sum_parts = const.tile([P, 2, 3], F32)
         twice_sums = const.tile([P, 2, len(TWICE_HIGH)], F32)
-        once_bank = psum_acc.tile([P, GROUP_ROWS], F32, name="acc")
-        gpsimd_bank = psum_acc.tile([P, GROUP_ROWS], F32, name="acc")
+        early_bank = psum_acc.tile([P, GROUP_ROWS], F32, name="acc")
+        late_bank = psum_acc.tile([P, GROUP_ROWS], F32, name="acc")
         row_squares = const.tile([P, GROUP, K], F32)
         more_squares = const.tile([P, GROUP, K], F32)
         gamma_mean = const.tile([P, 2, PACK], F32)
@@ -159,11 +156,13 @@ def tile_customnetwork_pa_t_kernel(tc, h_lin, gamma, beta, w, b, out):
         def merge_early(u, calls):
             for e in range(2):
                 nc.vector.bn_aggr(out=stats[:, u, merged, e, 1:3], in_=stats[:, u, 0:calls, e, :])
-            nc.scalar.activation(
+            nc.gpsimd.tensor_scalar(
                 out=stats[:, u, merged, :, 2],
-                in_=stats[:, u, merged, :, 2],
-                func=FUNC.Copy,
-                scale=float(early_rows[u]),
+                in0=stats[:, u, merged, :, 2],
+                scalar1=float(early_rows[u]),
+                scalar2=0.0,
+                op0=ALU.mult,
+                op1=ALU.add,
             )
 
         def squares_on_gpsimd(g):
@@ -181,9 +180,9 @@ def tile_customnetwork_pa_t_kernel(tc, h_lin, gamma, beta, w, b, out):
                         op=ALU.add,
                     )
 
-        def sum_columns(bank, column, count, part):
+        def sum_columns(out, bank, column, count):
             nc.vector.tensor_reduce(
-                out=sum_parts[:, :, part],
+                out=out[:],
                 in_=bank[:, column * ONES : (column + 2 * count) * ONES].rearrange(
                     "p (i e o) -> p e i o", e=2, o=ONES
                 )[:, :, :, 0],
@@ -191,45 +190,64 @@ def tile_customnetwork_pa_t_kernel(tc, h_lin, gamma, beta, w, b, out):
                 op=ALU.add,
             )
 
-        def close_gpsimd_and_scalar():
-            base = len(GPSIMD_GROUPS) * PACK * ONES
-            g_mean = stats[:, :, gpsimd_slot, :, 1]
-            sum_columns(gpsimd_bank, late_column, len(ONCE_HIGH) - early_once, 2)
+        def scale_on_gpsimd(out, in_, factor):
+            nc.gpsimd.tensor_scalar(out=out, in0=in_, scalar1=factor, scalar2=0.0, op0=ALU.mult, op1=ALU.add)
+
+        g_squares = const.tile([P, 2, 2], F32)
+        g_mean_sums = const.tile([P, 2, 2], F32)
+        share = const.tile([P, 2], F32)
+        off_share = const.tile([P, 2], F32)
+
+        def open_entries():
             g_sums = const.tile([P, 2, 2], F32)
+            columns = slice(gpsimd_column * ONES, (gpsimd_column + len(GPSIMD_GROUPS) * PACK) * ONES)
             nc.vector.tensor_reduce(
                 out=g_sums[:],
-                in_=gpsimd_bank[:, 0:base].rearrange("p (g u e o) -> p u e g o", u=2, e=2, o=ONES)[:, :, :, :, 0],
+                in_=early_bank[:, columns].rearrange("p (g u e o) -> p u e g o", u=2, e=2, o=ONES)[:, :, :, :, 0],
                 axis=AXIS.X,
                 op=ALU.add,
             )
-            sums = const.tile([P, 2], F32, name="s_sums")
-            nc.vector.tensor_reduce(out=sums[:], in_=sum_parts[:], axis=AXIS.X, op=ALU.add)
-            nc.vector.tensor_scalar(out=g_mean, in0=g_sums[:], scalar1=1.0 / gpsimd_rows, scalar2=None, op0=ALU.mult)
-            off = const.tile([P, 2], F32)
-            nc.vector.scalar_tensor_tensor(
-                out=off[:], in0=sums[:], scalar=1.0 / scalar_rows, in1=neg_shift[:], op0=ALU.mult, op1=ALU.add
-            )
-            nc.vector.tensor_scalar(
-                out=stats[:, 1, scalar_slot, :, 1], in0=sums[:], scalar1=1.0 / scalar_rows, scalar2=None, op0=ALU.mult
-            )
-            off_sq = const.tile([P, 2], F32)
-            nc.vector.tensor_tensor(out=off_sq[:], in0=off[:], in1=off[:], op=ALU.mult)
-            squares = const.tile([P, 2], F32, name="s_squares")
+            once = const.tile([P, 2], F32)
+            sum_columns(once, early_bank, 0, early_once)
+            twice = const.tile([P, 2], F32)
+            nc.vector.tensor_reduce(out=twice[:], in_=twice_sums[:], axis=AXIS.X, op=ALU.add)
+
+            g_mean = stats[:, :, gpsimd_slot, :, 1]
+            scale_on_gpsimd(g_mean, g_sums[:], 1.0 / gpsimd_rows)
+            nc.gpsimd.tensor_tensor(out=g_mean_sums[:], in0=g_mean, in1=g_sums[:], op=ALU.mult)
+            sums = const.tile([P, 2], F32)
+            nc.gpsimd.tensor_tensor(out=sums[:], in0=once[:], in1=twice[:], op=ALU.add)
+            scale_on_gpsimd(share[:], sums[:], 1.0 / scalar_rows)
+            nc.gpsimd.tensor_tensor(out=off_share[:], in0=share[:], in1=neg_shift[:], op=ALU.add)
+            scale_on_gpsimd(w_grouped[:], w_planes[:].rearrange("p t n -> p n t"), 1.0)
+
+        def close_entries():
+            late = const.tile([P, 2], F32)
+            sum_columns(late, late_bank, 0, len(ONCE_HIGH) - early_once)
+            squares = const.tile([P, 2], F32)
             nc.vector.tensor_reduce(
                 out=squares[:], in_=square_sums[:, :, 0 : len(SCALAR_HIGH) - 1], axis=AXIS.X, op=ALU.add
             )
-            g_mean_sums = const.tile([P, 2, 2], F32)
-            nc.vector.tensor_tensor(out=g_mean_sums[:], in0=g_mean, in1=g_sums[:], op=ALU.mult)
+            off = const.tile([P, 2], F32)
+            for total, early in ((off[:], off_share), (stats[:, 1, scalar_slot, :, 1], share)):
+                nc.vector.scalar_tensor_tensor(
+                    out=total, in0=late[:], scalar=1.0 / scalar_rows, in1=early[:], op0=ALU.mult, op1=ALU.add
+                )
+            off_sq = const.tile([P, 2], F32)
+            nc.vector.tensor_tensor(out=off_sq[:], in0=off[:], in1=off[:], op=ALU.mult)
+            g_spread = const.tile([P, 2, 2], F32)
+            nc.vector.tensor_tensor(
+                out=g_spread[:],
+                in0=g_squares[:],
+                in1=g_mean_sums[:],
+                op=ALU.subtract,
+            )
             spread = const.tile([P, 2], F32)
             nc.vector.scalar_tensor_tensor(
                 out=spread[:], in0=off_sq[:], scalar=-float(scalar_rows), in1=squares[:], op0=ALU.mult, op1=ALU.add
             )
-            g_spread = const.tile([P, 2, 2], F32)
-            nc.vector.tensor_tensor(
-                out=g_spread[:],
-                in0=gpsimd_bank[:, base : base + PACK * ONES].rearrange("p (u e o) -> p u e o", u=2, o=ONES)[:, :, :, 0],
-                in1=g_mean_sums[:],
-                op=ALU.subtract,
+            nc.vector.tensor_scalar(
+                out=stats[:, :, gpsimd_slot, :, 2], in0=g_spread[:], scalar1=0.0, scalar2=None, op0=ALU.max
             )
             nc.vector.tensor_tensor(
                 out=stats[:, 1, scalar_slot, :, 2],
@@ -237,30 +255,16 @@ def tile_customnetwork_pa_t_kernel(tc, h_lin, gamma, beta, w, b, out):
                 in1=square_sums[:, :, len(SCALAR_HIGH) - 1],
                 op=ALU.add,
             )
-            nc.vector.tensor_scalar(
-                out=stats[:, :, gpsimd_slot, :, 2], in0=g_spread[:], scalar1=0.0, scalar2=None, op0=ALU.max
-            )
 
         waiting_sums = []
         for g in range(GROUPS):
             if g in GPSIMD_GROUPS:
                 squares_on_gpsimd(g)
                 for t in range(PACK):
-                    waiting_sums.append((gpsimd_bank, GPSIMD_GROUPS.index(g) * PACK + t, g, t))
+                    waiting_sums.append((early_bank, gpsimd_column + GPSIMD_GROUPS.index(g) * PACK + t, g, t))
                 continue
             i = BANK_GROUPS.index(g)
             owner = owner_of_high(i)
-            if g == LAST:
-                for t in range(PACK):
-                    nc.tensor.matmul(
-                        out=gpsimd_bank[
-                            :, (len(GPSIMD_GROUPS) * PACK + t) * ONES : (len(GPSIMD_GROUPS) * PACK + t + 1) * ONES
-                        ],
-                        lhsT=row_squares[:, 0, :].rearrange("p (m t) -> p m t", t=PACK)[:, :, t],
-                        rhs=ones_f32[:],
-                        start=True,
-                        stop=True,
-                    )
             if i == 0:
                 xt_high = transpose_half(g, 1)
                 nc.vector.bn_stats(
@@ -299,13 +303,29 @@ def tile_customnetwork_pa_t_kernel(tc, h_lin, gamma, beta, w, b, out):
                     else:
                         o = ONCE_HIGH.index(i)
                         if o < early_once:
-                            waiting_sums.append((once_bank, o * 2 + e, g, 2 + e))
+                            waiting_sums.append((early_bank, o * 2 + e, g, 2 + e))
                         else:
-                            waiting_sums.append((gpsimd_bank, late_column + (o - early_once) * 2 + e, g, 2 + e))
+                            waiting_sums.append((late_bank, (o - early_once) * 2 + e, g, 2 + e))
             if i % SUM_EVERY == SUM_EVERY - 1 or i > EARLY:
                 for bank, column, rows_of, t in waiting_sums:
                     column_sum(bank, column, rows_of, t)
                 waiting_sums.clear()
+            if g == LAST:
+                squares_t = psum_x.tile([P, GROUP_ROWS], F32, name="xt")
+                for t in range(PACK):
+                    nc.tensor.transpose(
+                        squares_t[:, t * P : (t + 1) * P],
+                        row_squares[:, 0, :].rearrange("p (m t) -> p m t", t=PACK)[:, :, t],
+                        ident[:],
+                    )
+                for t in range(PACK):
+                    summed = unread.tile([P, P], F32, name="summed")
+                    nc.scalar.activation(
+                        out=summed[:],
+                        in_=squares_t[:, t * P : (t + 1) * P],
+                        func=FUNC.Identity,
+                        accum_out=g_squares[:, t // 2, t % 2 : t % 2 + 1],
+                    )
             if i == 2:
                 gb_t = psum_x.tile([P, GROUP_ROWS], F32, name="xt")
                 for u in range(2):
@@ -316,20 +336,18 @@ def tile_customnetwork_pa_t_kernel(tc, h_lin, gamma, beta, w, b, out):
                     pairs = gb_t[:].bitcast(BF16)[:, 2 * u * P : 2 * u * P + 4]
                     nc.vector.tensor_copy(out=gamma_mean[:, 0, 2 * u : 2 * u + 2], in_=pairs[:, 0:2])
                     nc.vector.tensor_copy(out=beta_k[:, 2 * u : 2 * u + 2], in_=pairs[:, 2:4])
-                nc.scalar.copy(out=w_grouped[:], in_=w_planes[:].rearrange("p t n -> p n t"))
             if i == EARLY - 1:
                 merge_early(0, early_calls)
                 merge_early(1, early_high * BN_CALLS)
             if i == EARLY:
-                sum_columns(once_bank, 0, early_once, 0)
-                nc.vector.tensor_reduce(out=sum_parts[:, :, 1], in_=twice_sums[:], axis=AXIS.X, op=ALU.add)
+                open_entries()
 
         xt_of = {}
         for g in range(AHEAD):
             xt_of[g] = [transpose_half(g, 0), transpose_half(g, 1)]
 
         mean_var = const.tile([P, PACK, 2], F32)
-        close_gpsimd_and_scalar()
+        close_entries()
         for e in range(2):
             nc.vector.bn_aggr(out=mean_var[:, 2 + e, :], in_=stats[:, 1, high_late : scalar_slot + 1, e, :])
         for e in range(2):

from contextlib import ExitStack

import concourse.masks as masks
import concourse.mybir as mybir

F32 = mybir.dt.float32
BF16 = mybir.dt.bfloat16
U32 = mybir.dt.uint32
U8 = mybir.dt.uint8
FP8X4 = mybir.dt.float8_e4m3fn_x4
FUNC = mybir.ActivationFunctionType
ALU = mybir.AluOpType
AXIS = mybir.AxisListType

P = 128
PACK = 4
ROWS = 16384
K = 512
N_OUT = 128
BN_EPS = 1e-5

BLOCKS = ROWS // P
GROUP = 4
GROUPS = BLOCKS // GROUP
GROUP_ROWS = GROUP * P
HALF_K = K // 2
BN_STATS_MAX = 512
BN_CALLS = 2 * GROUP_ROWS // BN_STATS_MAX
ONES = 2
AHEAD = 2

GPSIMD_GROUPS = (1, 5, 13, 21)
BANK_GROUPS = [g for g in range(GROUPS) if g not in GPSIMD_GROUPS]
LAST = BANK_GROUPS[-1]
SCALAR_INTERLEAVES = (GROUPS, GROUPS + 1)
SUM_EVERY = 4
EARLY = 24


def owner_of_high(i):
    if i % 5 == 4:
        return "vector"
    return "scalar_twice" if i % 5 == 1 and i < EARLY or i % 5 == 3 and i < 20 else "scalar"


VECTOR_HIGH = [i for i in range(len(BANK_GROUPS)) if owner_of_high(i) == "vector"]
SCALAR_HIGH = [i for i in range(len(BANK_GROUPS)) if owner_of_high(i) != "vector"]
TWICE_HIGH = [i for i in range(len(BANK_GROUPS)) if owner_of_high(i) == "scalar_twice"]
ONCE_HIGH = [i for i in range(len(BANK_GROUPS)) if owner_of_high(i) == "scalar"]

FLOPS = 2 * ROWS * K * N_OUT


def tile_customnetwork_pa_t_kernel(tc, h_lin, gamma, beta, w, b, out):
    nc = tc.nc
    x_dram = h_lin.rearrange("(p a) k -> p a k", a=BLOCKS)
    out_dram = out.rearrange("(p a) n -> p a n", a=BLOCKS)

    with ExitStack() as stack:
        const = stack.enter_context(tc.tile_pool(name="const", bufs=1))
        resident = stack.enter_context(tc.tile_pool(name="resident", bufs=GROUPS))
        unread = stack.enter_context(tc.tile_pool(name="unread", bufs=4))
        stage = stack.enter_context(tc.tile_pool(name="stage", bufs=4))
        results = stack.enter_context(tc.tile_pool(name="results", bufs=4))
        psum_x = stack.enter_context(tc.psum_pool(name="psum_x", bufs=6))
        psum_acc = stack.enter_context(tc.psum_pool(name="psum_acc", bufs=2))
        stack.enter_context(tc.manual_schedule())

        eps = const.tile([P, 1], F32)
        nc.vector.memset(eps[:], BN_EPS)
        ones = const.tile([P, ONES], BF16)
        nc.vector.memset(ones[:], 1.0)
        gb_rows = const.tile([P, K], BF16)
        nc.vector.memset(gb_rows[:], 0.0)
        ident = const.tile([P, P], F32)
        masks.make_identity(nc, ident[:])

        nc.scalar.dma_start(out=gb_rows[0:1, :], in_=gamma.unsqueeze(0))
        nc.scalar.dma_start(out=gb_rows[1:2, :], in_=beta.unsqueeze(0))
        w_planes = const.tile([P, PACK, N_OUT], BF16)
        nc.scalar.dma_start(out=w_planes[:], in_=w.rearrange("(p t) n -> p t n", t=PACK))
        warm = const.tile([P, 1], F32)
        nc.scalar.activation(out=warm[:], in_=eps[:], func=FUNC.Abs_reciprocal_sqrt)

        x_tiles = []
        for g in range(GROUPS):
            x_g = resident.tile([P, GROUP, K], BF16, name="x_g")
            if g == 0:
                for j in range(GROUP):
                    nc.sync.dma_start(out=x_g[:, j, :], in_=x_dram[:, j, :])
            else:
                nc.sync.dma_start(out=x_g[:], in_=x_dram[:, g * GROUP : (g + 1) * GROUP, :])
            x_tiles.append(x_g)
        b_rows = const.tile([P, N_OUT], BF16)
        nc.sync.dma_start(out=b_rows[:], in_=b.partition_broadcast(P))

        def transpose_half(g, u):
            words = x_tiles[g][:].bitcast(F32)
            xt = psum_x.tile([P, GROUP_ROWS], F32, name="xt")
            for j in range(GROUP):
                nc.tensor.transpose(
                    xt[:, j * P : (j + 1) * P], words[:, j, u : HALF_K : 2], ident[:]
                )
            return xt

        def one_k(xt, e, columns=slice(0, GROUP_ROWS)):
            return xt[:].bitcast(BF16).rearrange("p (r e) -> p r e", e=2)[:, columns, e]

        def column_sum(bank, column, g, t):
            for j in range(GROUP):
                nc.tensor.matmul(
                    out=bank[:, column * ONES : (column + 1) * ONES],
                    lhsT=x_tiles[g][:, j, :].rearrange("p (m t) -> p m t", t=PACK)[:, :, t],
                    rhs=ones[:],
                    start=(j == 0),
                    stop=(j == GROUP - 1),
                )

        low_calls = len(BANK_GROUPS) * BN_CALLS
        early_calls = EARLY * BN_CALLS
        early_high = len([i for i in VECTOR_HIGH if i < EARLY])
        high_late = low_calls - BN_CALLS * (len(VECTOR_HIGH) - early_high)
        merged, gpsimd_slot, scalar_slot = low_calls, low_calls + 1, low_calls + 2
        stats = const.tile([P, 2, low_calls + 4, 2, 3], F32)
        early_once = len([i for i in ONCE_HIGH if i < EARLY])
        gpsimd_column = early_once * 2
        early_rows = (EARLY * GROUP_ROWS, early_high * GROUP_ROWS)
        gpsimd_rows = len(GPSIMD_GROUPS) * GROUP_ROWS
        scalar_rows = len(SCALAR_HIGH) * GROUP_ROWS
        for u in range(2):
            nc.vector.memset(stats[:, u, merged, :, :], float(early_rows[u]))
        nc.vector.memset(stats[:, :, gpsimd_slot, :, :], float(gpsimd_rows))
        nc.vector.memset(stats[:, 1, scalar_slot, :, :], float(scalar_rows))

        shift_stats = const.tile([P, 2, 3], F32)
        neg_shift = const.tile([P, 2], F32)
        square_sums = const.tile([P, 2, len(SCALAR_HIGH)], F32)
        twice_sums = const.tile([P, 2, len(TWICE_HIGH)], F32)
        early_bank = psum_acc.tile([P, GROUP_ROWS], F32, name="acc")
        late_bank = psum_acc.tile([P, GROUP_ROWS], F32, name="acc")
        row_squares = const.tile([P, GROUP, K], F32)
        more_squares = const.tile([P, GROUP, K], F32)
        gamma_mean = const.tile([P, 2, PACK], F32)
        beta_k = const.tile([P, PACK], F32)
        w_grouped = const.tile([P, N_OUT, PACK], BF16, align_bytes=64)
        w_codes = const.tile([P, N_OUT], U32, align_bytes=64)
        w_scales = const.tile([P, N_OUT], U8, align_bytes=64)

        def bn_bank(xt, u, first_slot):
            for i in range(BN_CALLS):
                nc.vector.bn_stats(
                    out=stats[:, u, first_slot + i, :, :].rearrange("p e s -> p (e s)"),
                    in_=xt[:].bitcast(BF16)[:, i * BN_STATS_MAX : (i + 1) * BN_STATS_MAX],
                )

        def merge_early(u, calls):
            for e in range(2):
                nc.vector.bn_aggr(out=stats[:, u, merged, e, 1:3], in_=stats[:, u, 0:calls, e, :])
            nc.gpsimd.tensor_scalar(
                out=stats[:, u, merged, :, 2],
                in0=stats[:, u, merged, :, 2],
                scalar1=float(early_rows[u]),
                scalar2=0.0,
                op0=ALU.mult,
                op1=ALU.add,
            )

        def squares_on_gpsimd(g):
            first = g == GPSIMD_GROUPS[0]
            squares = row_squares if first else more_squares
            nc.gpsimd.tensor_tensor(out=squares[:], in0=x_tiles[g][:], in1=x_tiles[g][:], op=ALU.mult)
            if not first:
                nc.gpsimd.tensor_tensor(out=row_squares[:], in0=row_squares[:], in1=more_squares[:], op=ALU.add)
            if g == GPSIMD_GROUPS[-1]:
                for half in (2, 1):
                    nc.gpsimd.tensor_tensor(
                        out=row_squares[:, 0:half, :],
                        in0=row_squares[:, 0:half, :],
                        in1=row_squares[:, half : 2 * half, :],
                        op=ALU.add,
                    )

        def sum_columns(out, bank, column, count):
            nc.vector.tensor_reduce(
                out=out[:],
                in_=bank[:, column * ONES : (column + 2 * count) * ONES].rearrange(
                    "p (i e o) -> p e i o", e=2, o=ONES
                )[:, :, :, 0],
                axis=AXIS.X,
                op=ALU.add,
            )

        def scale_on_gpsimd(out, in_, factor):
            nc.gpsimd.tensor_scalar(out=out, in0=in_, scalar1=factor, scalar2=0.0, op0=ALU.mult, op1=ALU.add)

        g_squares = const.tile([P, 2, 2], F32)
        g_mean_sums = const.tile([P, 2, 2], F32)
        share = const.tile([P, 2], F32)
        off_share = const.tile([P, 2], F32)

        def open_entries():
            g_sums = const.tile([P, 2, 2], F32)
            columns = slice(gpsimd_column * ONES, (gpsimd_column + len(GPSIMD_GROUPS) * PACK) * ONES)
            nc.vector.tensor_reduce(
                out=g_sums[:],
                in_=early_bank[:, columns].rearrange("p (g u e o) -> p u e g o", u=2, e=2, o=ONES)[:, :, :, :, 0],
                axis=AXIS.X,
                op=ALU.add,
            )
            once = const.tile([P, 2], F32)
            sum_columns(once, early_bank, 0, early_once)
            twice = const.tile([P, 2], F32)
            nc.vector.tensor_reduce(out=twice[:], in_=twice_sums[:], axis=AXIS.X, op=ALU.add)

            g_mean = stats[:, :, gpsimd_slot, :, 1]
            scale_on_gpsimd(g_mean, g_sums[:], 1.0 / gpsimd_rows)
            nc.gpsimd.tensor_tensor(out=g_mean_sums[:], in0=g_mean, in1=g_sums[:], op=ALU.mult)
            sums = const.tile([P, 2], F32)
            nc.gpsimd.tensor_tensor(out=sums[:], in0=once[:], in1=twice[:], op=ALU.add)
            scale_on_gpsimd(share[:], sums[:], 1.0 / scalar_rows)
            nc.gpsimd.tensor_tensor(out=off_share[:], in0=share[:], in1=neg_shift[:], op=ALU.add)
            scale_on_gpsimd(w_grouped[:], w_planes[:].rearrange("p t n -> p n t"), 1.0)

        def close_entries():
            late = const.tile([P, 2], F32)
            sum_columns(late, late_bank, 0, len(ONCE_HIGH) - early_once)
            squares = const.tile([P, 2], F32)
            nc.vector.tensor_reduce(
                out=squares[:], in_=square_sums[:, :, 0 : len(SCALAR_HIGH) - 1], axis=AXIS.X, op=ALU.add
            )
            off = const.tile([P, 2], F32)
            for total, early in ((off[:], off_share), (stats[:, 1, scalar_slot, :, 1], share)):
                nc.vector.scalar_tensor_tensor(
                    out=total, in0=late[:], scalar=1.0 / scalar_rows, in1=early[:], op0=ALU.mult, op1=ALU.add
                )
            off_sq = const.tile([P, 2], F32)
            nc.vector.tensor_tensor(out=off_sq[:], in0=off[:], in1=off[:], op=ALU.mult)
            g_spread = const.tile([P, 2, 2], F32)
            nc.vector.tensor_tensor(
                out=g_spread[:],
                in0=g_squares[:],
                in1=g_mean_sums[:],
                op=ALU.subtract,
            )
            spread = const.tile([P, 2], F32)
            nc.vector.scalar_tensor_tensor(
                out=spread[:], in0=off_sq[:], scalar=-float(scalar_rows), in1=squares[:], op0=ALU.mult, op1=ALU.add
            )
            nc.vector.tensor_scalar(
                out=stats[:, :, gpsimd_slot, :, 2], in0=g_spread[:], scalar1=0.0, scalar2=None, op0=ALU.max
            )
            nc.vector.tensor_tensor(
                out=stats[:, 1, scalar_slot, :, 2],
                in0=spread[:],
                in1=square_sums[:, :, len(SCALAR_HIGH) - 1],
                op=ALU.add,
            )

        waiting_sums = []
        for g in range(GROUPS):
            if g in GPSIMD_GROUPS:
                squares_on_gpsimd(g)
                for t in range(PACK):
                    waiting_sums.append((early_bank, gpsimd_column + GPSIMD_GROUPS.index(g) * PACK + t, g, t))
                continue
            i = BANK_GROUPS.index(g)
            owner = owner_of_high(i)
            if i == 0:
                xt_high = transpose_half(g, 1)
                nc.vector.bn_stats(
                    out=shift_stats[:].rearrange("p e s -> p (e s)"), in_=xt_high[:].bitcast(BF16)[:, 0 : 2 * P]
                )
                nc.scalar.activation(out=neg_shift[:], in_=shift_stats[:, :, 1], func=FUNC.Copy, scale=-1.0)
                xt_low = transpose_half(g, 0)
            else:
                xt_low = transpose_half(g, 0)
                xt_high = transpose_half(g, 1)
            bn_bank(xt_low, 0, i * BN_CALLS)
            if owner == "vector":
                v = VECTOR_HIGH.index(i)
                bn_bank(xt_high, 1, v * BN_CALLS if i < EARLY else high_late + (v - early_high) * BN_CALLS)
            else:
                s = SCALAR_HIGH.index(i)
                for e in range(2):
                    squares = unread.tile([P, GROUP_ROWS], BF16, name="squares")
                    nc.scalar.activation(
                        out=squares[:],
                        in_=one_k(xt_high, e),
                        func=FUNC.Square,
                        bias=neg_shift[:, e : e + 1],
                        scale=1.0,
                        accum_out=square_sums[:, e, s : s + 1],
                    )
                    if owner == "scalar_twice":
                        d = TWICE_HIGH.index(i)
                        copy = unread.tile([P, GROUP_ROWS], BF16, name="squares")
                        nc.scalar.activation(
                            out=copy[:],
                            in_=one_k(xt_high, e),
                            func=FUNC.Identity,
                            accum_out=twice_sums[:, e, d : d + 1],
                        )
                    else:
                        o = ONCE_HIGH.index(i)
                        if o < early_once:
                            waiting_sums.append((early_bank, o * 2 + e, g, 2 + e))
                        else:
                            waiting_sums.append((late_bank, (o - early_once) * 2 + e, g, 2 + e))
            if i % SUM_EVERY == SUM_EVERY - 1 or i > EARLY:
                for bank, column, rows_of, t in waiting_sums:
                    column_sum(bank, column, rows_of, t)
                waiting_sums.clear()
            if g == LAST:
                squares_t = psum_x.tile([P, GROUP_ROWS], F32, name="xt")
                for t in range(PACK):
                    nc.tensor.transpose(
                        squares_t[:, t * P : (t + 1) * P],
                        row_squares[:, 0, :].rearrange("p (m t) -> p m t", t=PACK)[:, :, t],
                        ident[:],
                    )
                for t in range(PACK):
                    summed = unread.tile([P, P], F32, name="summed")
                    nc.scalar.activation(
                        out=summed[:],
                        in_=squares_t[:, t * P : (t + 1) * P],
                        func=FUNC.Identity,
                        accum_out=g_squares[:, t // 2, t % 2 : t % 2 + 1],
                    )
            if i == 2:
                gb_t = psum_x.tile([P, GROUP_ROWS], F32, name="xt")
                for u in range(2):
                    nc.tensor.transpose(
                        gb_t[:, u * P : (u + 1) * P], gb_rows[:].bitcast(F32)[:, u : HALF_K : 2], ident[:]
                    )
                for u in range(2):
                    pairs = gb_t[:].bitcast(BF16)[:, 2 * u * P : 2 * u * P + 4]
                    nc.vector.tensor_copy(out=gamma_mean[:, 0, 2 * u : 2 * u + 2], in_=pairs[:, 0:2])
                    nc.vector.tensor_copy(out=beta_k[:, 2 * u : 2 * u + 2], in_=pairs[:, 2:4])
            if i == EARLY - 1:
                merge_early(0, early_calls)
                merge_early(1, early_high * BN_CALLS)
            if i == EARLY:
                open_entries()

        xt_of = {}
        for g in range(AHEAD):
            xt_of[g] = [transpose_half(g, 0), transpose_half(g, 1)]

        mean_var = const.tile([P, PACK, 2], F32)
        close_entries()
        for e in range(2):
            nc.vector.bn_aggr(out=mean_var[:, 2 + e, :], in_=stats[:, 1, high_late : scalar_slot + 1, e, :])
        for e in range(2):
            nc.vector.bn_aggr(out=mean_var[:, e, :], in_=stats[:, 0, early_calls : gpsimd_slot + 1, e, :])
        inv_std = const.tile([P, PACK], F32)
        nc.scalar.activation(
            out=inv_std[:], in_=mean_var[:, :, 1], func=FUNC.Abs_reciprocal_sqrt, bias=eps[:], scale=1.0
        )
        nc.vector.tensor_tensor(
            out=gamma_mean[:, 1, :], in0=gamma_mean[:, 0, :], in1=mean_var[:, :, 0], op=ALU.mult
        )
        scaled = const.tile([P, 2, PACK], F32)
        nc.vector.tensor_tensor(
            out=scaled[:],
            in0=gamma_mean[:],
            in1=inv_std[:].unsqueeze(1).to_broadcast([P, 2, PACK]),
            op=ALU.mult,
        )
        offset_k = const.tile([P, PACK], F32)
        nc.vector.tensor_tensor(out=offset_k[:], in0=beta_k[:], in1=scaled[:, 1, :], op=ALU.subtract)

        halves = [(0, GROUP // 2), (GROUP // 2, GROUP // 2)]
        chunks = [(0, *half) for half in halves]
        chunks += [(g, 0, GROUP) for g in range(1, GROUPS - 1)]
        chunks += [(GROUPS - 1, *half) for half in halves]
        last = len(chunks) - 1
        planes_of = {}
        grouped_of = {}
        acc_of = {}

        def normalise(s):
            g, first, count = chunks[s]
            rows = count * P
            columns = slice(first * P, first * P + rows)
            planes = stage.tile([P, PACK, rows], BF16, name="planes")
            for u in range(2):
                for e in range(2):
                    t = 2 * u + e
                    scale = scaled[:, 0, t : t + 1]
                    offset = offset_k[:, t : t + 1]
                    if g == 0 and u == 1:
                        nc.vector.tensor_scalar(
                            out=planes[:, t, :],
                            in0=one_k(xt_of[g][u], e, columns),
                            scalar1=scale,
                            scalar2=offset,
                            op0=ALU.mult,
                            op1=ALU.add,
                        )
                    else:
                        nc.scalar.activation(
                            out=planes[:, t, :],
                            in_=one_k(xt_of[g][u], e, columns),
                            func=FUNC.Relu,
                            bias=offset,
                            scale=scale,
                        )
            planes_of[s] = planes

        def interleave(s):
            rows = chunks[s][2] * P
            grouped = stage.tile([P, rows, PACK], BF16, name="grouped", align_bytes=64)
            target = grouped[:].rearrange("p (c i) t -> p c t i", i=4)
            source = planes_of[s][:].rearrange("p t (c i) -> p c t i", i=4)
            if chunks[s][0] == 0:
                nc.vector.tensor_scalar(out=target, in0=source, scalar1=0.0, scalar2=None, op0=ALU.max)
            elif s in SCALAR_INTERLEAVES:
                nc.scalar.copy(out=target, in_=source)
            else:
                nc.vector.tensor_copy(out=target, in_=source)
            grouped_of[s] = grouped

        def quantise_and_multiply(s):
            count = chunks[s][2]
            rows = count * P
            codes = stage.tile([P, rows], U32, name="codes", align_bytes=64)
            scales = stage.tile([P, rows], U8, name="scales", align_bytes=64)
            nc.vector.quantize_mx(
                out=codes[:].bitcast(FP8X4),
                scales=scales[:],
                in_=grouped_of[s][:].rearrange("p r t -> p (r t)"),
            )
            acc = psum_acc.tile([P, count, N_OUT], F32, name="acc")
            for j in range(count):
                block = slice(j * P, (j + 1) * P)
                nc.tensor.matmul_mx(
                    out=acc[:, j, :],
                    lhsT=codes[:, block].bitcast(FP8X4),
                    lhsT_scale=scales[:, block],
                    rhs=w_codes[:].bitcast(FP8X4),
                    rhs_scale=w_scales[:],
                    start=True,
                    stop=True,
                )
            acc_of[s] = acc

        def add_bias_and_store(s):
            g, first, count = chunks[s]
            result = results.tile([P, count, N_OUT], F32, name="result")
            nc.vector.tensor_tensor(
                out=result[:],
                in0=acc_of[s][:],
                in1=b_rows[:].unsqueeze(1).to_broadcast([P, count, N_OUT]),
                op=ALU.add,
            )
            a0 = g * GROUP + first
            nc.sync.dma_start(out=out_dram[:, a0 : a0 + count, :], in_=result[:])

        for s in range(len(chunks)):
            g, first, count = chunks[s]
            if first == 0 and g + AHEAD < GROUPS:
                xt_of[g + AHEAD] = [transpose_half(g + AHEAD, 0), transpose_half(g + AHEAD, 1)]
            normalise(s)
            interleave(s)
            if s == 0:
                nc.vector.quantize_mx(
                    out=w_codes[:].bitcast(FP8X4),
                    scales=w_scales[:],
                    in_=w_grouped[:].rearrange("p n t -> p (n t)"),
                )
            if s >= 1:
                quantise_and_multiply(s - 1)
            if s >= 2:
                add_bias_and_store(s - 2)
        quantise_and_multiply(last)
        add_bias_and_store(last - 1)
        add_bias_and_store(last)
